import numpy as np
import ml_dtypes


def mxq(x, axis, fmt="e4m3"):
    dtype, down = {"e4m3": (ml_dtypes.float8_e4m3fn, 7), "e5m2": (ml_dtypes.float8_e5m2, 14)}[fmt]
    v = np.moveaxis(np.asarray(x, np.float32).astype(ml_dtypes.bfloat16).astype(np.float64), axis, -1)
    blocks = v.reshape(v.shape[:-1] + (-1, 32))
    amax = np.abs(blocks).max(-1, keepdims=True)
    byte = np.maximum(np.where(amax > 0, np.frexp(amax)[1] - 1 + 127, 0) - down, 1)
    scale = np.exp2(byte - 127.0)
    codes = (blocks / scale).astype(np.float32).astype(dtype).astype(np.float64)
    return np.moveaxis((codes * scale).reshape(v.shape), -1, axis)


WIDE = False


def mx_kscale(k):
    if not WIDE:
        return np.ones(k)
    levels = np.array([10, -10, 5, -5, 0])
    a = np.random.permutation(np.resize(levels, k // 512 * 4)).reshape(k // 512, 4)
    idx = np.arange(k)
    return np.exp2(a[idx // 512, idx % 128 // 32])


BF16 = ml_dtypes.bfloat16


def bf(x):
    return np.asarray(x, np.float32).astype(BF16)


def f64(x):
    return np.asarray(x).astype(np.float64)


N, B, K, E, IN, C = 4, 128, 1024, 256, 784, 128
BETA = 2.0
SK = 0.6
SQ = 0.7 * np.sqrt(2.0 * np.log(K)) / (BETA * SK * np.sqrt(E))


def setup_inputs():
    t = mx_kscale(N * E).reshape(N, E)
    return {
        "q_state": bf(np.random.standard_normal((N, B, E)) * SQ / t[:, None, :]),
        "keys": bf(np.random.standard_normal((N, K, E)) * SK * t[:, None, :]),
        "W_lin": bf(np.random.standard_normal((N * E, C)) * 6.0 / np.sqrt(N * E) / t.reshape(N * E, 1)),
        "b_lin": bf(np.random.standard_normal(C) * 0.5),
    }


def reference(q_state, keys, W_lin, b_lin):
    kk = f64(keys)
    s = BETA * (f64(q_state) @ kk.transpose(0, 2, 1))
    e = np.exp(s - s.max(-1, keepdims=True))
    r = (mxq(e, 2, "e4m3") @ mxq(kk, 1, "e4m3")) / e.sum(-1, keepdims=True)
    h = np.maximum(r.transpose(1, 0, 2).reshape(B, N * E), 0.0)
    y = (mxq(h, 1, "e4m3") @ mxq(f64(W_lin), 0, "e4m3")) + f64(b_lin)
    y = y - y.max(-1, keepdims=True)
    return y - np.log(np.exp(y).sum(-1, keepdims=True))

@@ -1,0 +1,300 @@
+from contextlib import ExitStack
+
+import concourse.mybir as mybir
+from concourse.masks import make_identity
+
+F32 = mybir.dt.float32
+BF16 = mybir.dt.bfloat16
+U32 = mybir.dt.uint32
+U8 = mybir.dt.uint8
+FP8X4 = mybir.dt.float8_e4m3fn_x4
+ACT = mybir.ActivationFunctionType
+ALU = mybir.AluOpType
+AX = mybir.AxisListType
+
+NETS, B, K, E, C = 4, 128, 1024, 256, 128
+BETA = 2.0
+P = 128
+PACK = 4
+K_PASS = P * PACK
+PASSES = K // K_PASS
+E_HALVES = E // P
+AHEAD = 2
+
+FLOPS = 2 * NETS * B * K * E * 2 + 2 * B * NETS * E * C
+
+
+def tile_hopfieldmodel_pa_s_kernel(tc, q_state, keys, W_lin, b_lin, out):
+    nc = tc.nc
+    with ExitStack() as ctx:
+        const = ctx.enter_context(tc.tile_pool(name="const", bufs=1))
+        per_net = ctx.enter_context(tc.tile_pool(name="per_net", bufs=NETS))
+        ps_t = ctx.enter_context(tc.psum_pool(name="ps_t", bufs=2))
+        ps_s = ctx.enter_context(tc.psum_pool(name="ps_s", bufs=2 * PASSES))
+        ctx.enter_context(tc.manual_schedule())
+
+        keys_sb = [
+            const.tile([P, PASSES, PACK, E], BF16, name="keys_sb%d" % n) for n in range(NETS)
+        ]
+        q_sb = const.tile([P, NETS, E], BF16)
+        w_sb = const.tile([P, PASSES, PACK, C], BF16)
+        bias_sb = const.tile([P, C], BF16)
+
+        def keys_view(n):
+            return keys[n].rearrange("(g p j) e -> p g j e", g=PASSES, j=PACK)
+
+        nc.sync.dma_start(out=keys_sb[0][:, 0], in_=keys_view(0)[:, 0])
+        nc.sync.dma_start(out=q_sb[:], in_=q_state.rearrange("n b e -> b n e"))
+        nc.sync.dma_start(out=keys_sb[0][:, 1], in_=keys_view(0)[:, 1])
+        for n in range(1, NETS):
+            nc.sync.dma_start(out=keys_sb[n][:], in_=keys_view(n))
+        nc.sync.dma_start(
+            out=w_sb[:], in_=W_lin.rearrange("(g t p) c -> p g t c", g=PASSES, t=PACK)
+        )
+        nc.sync.dma_start(out=bias_sb[:], in_=b_lin.partition_broadcast(P))
+
+        ident = const.tile([P, P], F32)
+        make_identity(nc, ident[:])
+
+        q_t = const.tile([P, NETS, B], F32)
+        keys_t = [const.tile([P, PASSES, K_PASS], F32, name="keys_t%d" % n) for n in range(NETS)]
+        bank_sum = const.tile([P, NETS, PASSES], F32)
+        scores, neg_max, e_sb, e_grouped = {}, {}, {}, {}
+        k_codes, k_scales, e_codes, e_scales, retrieved = {}, {}, {}, {}, {}
+
+        def transpose_q():
+            qt_ps = ps_t.tile([P, NETS, B], F32, tag="et")
+            for n in range(NETS):
+                nc.tensor.transpose(
+                    out=qt_ps[:, n, :], in_=q_sb[:, n, :].bitcast(F32), identity=ident[:]
+                )
+            nc.scalar.copy(out=q_t[:], in_=qt_ps[:])
+
+        def transpose_keys(n, g):
+            kt_ps = ps_t.tile([P, PACK, P], F32, tag="kt")
+            for j in range(PACK):
+                nc.tensor.transpose(
+                    out=kt_ps[:, j, :], in_=keys_sb[n][:, g, j, :].bitcast(F32), identity=ident[:]
+                )
+            return kt_ps
+
+        def store_keys_t(n, g, kt_ps):
+            nc.scalar.copy(
+                out=keys_t[n][:, g, :].rearrange("w (u p i) -> w u p i", u=2, i=2),
+                in_=kt_ps[:].rearrange("w (u i) p -> w u p i", i=2),
+            )
+
+        def score(n, g):
+            s_ps = ps_s.tile([P, K_PASS], F32, tag="s")
+            for parity in range(2):
+                nc.tensor.matmul(
+                    out=s_ps[:],
+                    lhsT=q_t[:, n, :].bitcast(BF16).rearrange("w (b i) -> w b i", i=2)[
+                        :, :, parity
+                    ],
+                    rhs=keys_t[n][:, g, :].bitcast(BF16).rearrange("w (c i) -> w c i", i=2)[
+                        :, :, parity
+                    ],
+                    start=(parity == 0),
+                    stop=(parity == 1),
+                )
+            scores[(n, g)] = s_ps
+
+        def row_max(n):
+            bank_max = per_net.tile([P, PASSES], F32, tag="bank_max")
+            for g in range(PASSES):
+                nc.vector.tensor_reduce(
+                    out=bank_max[:, g : g + 1], in_=scores[(n, g)][:], axis=AX.X, op=ALU.max
+                )
+            neg_max[n] = per_net.tile([P, 1], F32, tag="neg_max", name="neg_max")
+            nc.vector.tensor_scalar(
+                out=neg_max[n][:],
+                in0=bank_max[:, 0:1],
+                scalar1=bank_max[:, 1:2],
+                scalar2=-BETA,
+                op0=ALU.max,
+                op1=ALU.mult,
+            )
+
+        def exponentiate(n):
+            e_sb[n] = per_net.tile([P, PASSES, K_PASS], BF16, tag="e_sb", name="e_sb")
+            for g in range(PASSES):
+                nc.scalar.activation(
+                    out=e_sb[n][:, g, :],
+                    in_=scores[(n, g)][:],
+                    func=ACT.Exp,
+                    bias=neg_max[n][:],
+                    scale=BETA,
+                    accum_out=bank_sum[:, n, g : g + 1],
+                )
+
+        def transpose_e(n, g):
+            et_ps = ps_t.tile([P, 2, B], F32, tag="et")
+            for u in range(2):
+                nc.tensor.transpose(
+                    out=et_ps[:, u, :],
+                    in_=e_sb[n][:, g, :].bitcast(F32)[:, u * P : (u + 1) * P],
+                    identity=ident[:],
+                )
+            return et_ps
+
+        def store_e_t(n, g, et_ps):
+            if g == 0:
+                e_grouped[n] = per_net.tile(
+                    [P, PASSES, B, PACK], BF16, align_bytes=64, tag="e_grouped", name="e_grouped"
+                )
+            nc.scalar.copy(
+                out=e_grouped[n][:, g].rearrange("p b j -> p (b j)").bitcast(F32).rearrange(
+                    "p (b u) -> p b u", u=2
+                ),
+                in_=et_ps[:].rearrange("p u b -> p b u"),
+            )
+
+        def quantise_keys(n):
+            grouped = per_net.tile([P, PASSES, E, PACK], BF16, align_bytes=64, tag="k_grouped")
+            for g in range(PASSES):
+                nc.vector.tensor_copy(
+                    out=grouped[:, g].rearrange("p (c i) j -> p c j i", i=4),
+                    in_=keys_sb[n][:, g].rearrange("p j (c i) -> p c j i", i=4),
+                )
+            k_codes[n] = per_net.tile([P, PASSES, E], U32, align_bytes=64, tag="k_codes", name="kc")
+            k_scales[n] = per_net.tile([P, PASSES, E], U8, align_bytes=64, tag="k_scales", name="ks")
+            nc.vector.quantize_mx(
+                out=k_codes[n][:].rearrange("p g e -> p (g e)").bitcast(FP8X4),
+                scales=k_scales[n][:].rearrange("p g e -> p (g e)"),
+                in_=grouped[:].rearrange("p g e j -> p (g e j)"),
+            )
+
+        def quantise_e(n):
+            e_codes[n] = per_net.tile([P, PASSES, B], U32, align_bytes=64, tag="e_codes", name="ec")
+            e_scales[n] = per_net.tile([P, PASSES, B], U8, align_bytes=64, tag="e_scales", name="es")
+            nc.vector.quantize_mx(
+                out=e_codes[n][:].rearrange("p g b -> p (g b)").bitcast(FP8X4),
+                scales=e_scales[n][:].rearrange("p g b -> p (g b)"),
+                in_=e_grouped[n][:].rearrange("p g b j -> p (g b j)"),
+            )
+
+        def retrieve(n):
+            rt_ps = ps_s.tile([P, E_HALVES, B], F32, tag="s")
+            for half in range(E_HALVES):
+                cols = slice(half * P, (half + 1) * P)
+                for g in range(PASSES):
+                    nc.tensor.matmul_mx(
+                        out=rt_ps[:, half, :],
+                        lhsT=k_codes[n][:, g, cols].bitcast(FP8X4),
+                        lhsT_scale=k_scales[n][:, g, cols],
+                        rhs=e_codes[n][:, g, :].bitcast(FP8X4),
+                        rhs_scale=e_scales[n][:, g, :],
+                        start=(g == 0),
+                        stop=(g == PASSES - 1),
+                    )
+            retrieved[n] = rt_ps
+
+        store_keys_t(0, 0, transpose_keys(0, 0))
+        transpose_q()
+        store_keys_t(0, 1, transpose_keys(0, 1))
+        for g in range(PASSES):
+            score(0, g)
+            store_keys_t(1, g, transpose_keys(1, g))
+        for g in range(PASSES):
+            score(1, g)
+        quantise_keys(0)
+        row_max(0)
+
+        for n in range(NETS):
+            exponentiate(n)
+            ahead = n + AHEAD
+            if ahead < NETS:
+                kt_banks = [transpose_keys(ahead, g) for g in range(PASSES)]
+            et_banks = [transpose_e(n, g) for g in range(PASSES)]
+            if ahead < NETS:
+                for g in range(PASSES):
+                    store_keys_t(ahead, g, kt_banks[g])
+                    score(ahead, g)
+            for g in range(PASSES):
+                store_e_t(n, g, et_banks[g])
+            if n + 1 < NETS:
+                row_max(n + 1)
+                quantise_keys(n + 1)
+
+        row_sum = const.tile([P, NETS], F32)
+        nc.vector.tensor_reduce(out=row_sum[:], in_=bank_sum[:], axis=AX.X, op=ALU.add)
+        inv_sum = const.tile([P, NETS], F32)
+        nc.vector.reciprocal(out=inv_sum[:], in_=row_sum[:])
+        spread_ps = ps_t.tile([P, NETS, B], F32, tag="kt")
+        for n in range(NETS):
+            nc.tensor.transpose(
+                out=spread_ps[:, n, :],
+                in_=inv_sum[:, n : n + 1].to_broadcast([P, P]),
+                identity=ident[:],
+            )
+        inv_spread = const.tile([P, NETS, B], F32)
+        nc.scalar.copy(out=inv_spread[:], in_=spread_ps[:])
+
+        w_grouped = const.tile([P, PASSES, C, PACK], BF16, align_bytes=64)
+        nc.scalar.copy(out=w_grouped[:], in_=w_sb[:].rearrange("p g t c -> p g c t"))
+        w_codes = const.tile([P, PASSES, C], U32, align_bytes=64)
+        w_scales = const.tile([P, PASSES, C], U8, align_bytes=64)
+
+        for n in range(NETS):
+            quantise_e(n)
+            retrieve(n)
+
+        h_grouped = const.tile([P, PASSES, B, PACK], BF16, align_bytes=64)
+        h_codes = const.tile([P, PASSES, B], U32, align_bytes=64)
+        h_scales = const.tile([P, PASSES, B], U8, align_bytes=64)
+        for n in range(NETS):
+            if n == NETS - 1:
+                nc.vector.quantize_mx(
+                    out=w_codes[:].rearrange("p g c -> p (g c)").bitcast(FP8X4),
+                    scales=w_scales[:].rearrange("p g c -> p (g c)"),
+                    in_=w_grouped[:].rearrange("p g c t -> p (g c t)"),
+                )
+            t0 = E_HALVES * (n % 2)
+            nc.vector.scalar_tensor_tensor(
+                out=h_grouped[:, n // 2, :, t0 : t0 + E_HALVES],
+                in0=retrieved[n][:].rearrange("p t b -> p b t"),
+                scalar=0.0,
+                in1=inv_spread[:, n, :].unsqueeze(2).to_broadcast([P, B, E_HALVES]),
+                op0=ALU.max,
+                op1=ALU.mult,
+            )
+            if n % 2 == 1:
+                g = n // 2
+                nc.vector.quantize_mx(
+                    out=h_codes[:, g, :].bitcast(FP8X4),
+                    scales=h_scales[:, g, :],
+                    in_=h_grouped[:, g].rearrange("p b t -> p (b t)"),
+                )
+
+        y_ps = ps_s.tile([P, C], F32, tag="s")
+        for g in range(PASSES):
+            nc.tensor.matmul_mx(
+                out=y_ps[:],
+                lhsT=h_codes[:, g, :].bitcast(FP8X4),
+                lhsT_scale=h_scales[:, g, :],
+                rhs=w_codes[:, g, :].bitcast(FP8X4),
+                rhs_scale=w_scales[:, g, :],
+                start=(g == 0),
+                stop=(g == PASSES - 1),
+            )
+        y = const.tile([P, C], F32)
+        nc.vector.tensor_tensor(out=y[:], in0=y_ps[:], in1=bias_sb[:], op=ALU.add)
+        y_max = const.tile([P, 1], F32)
+        nc.vector.tensor_reduce(out=y_max[:], in_=y[:], axis=AX.X, op=ALU.max)
+        shifted = const.tile([P, C], F32)
+        nc.vector.tensor_scalar(
+            out=shifted[:], in0=y[:], scalar1=y_max[:], scalar2=None, op0=ALU.subtract
+        )
+        exp_shifted = const.tile([P, C], F32)
+        exp_sum = const.tile([P, 1], F32)
+        nc.scalar.activation(
+            out=exp_shifted[:], in_=shifted[:], func=ACT.Exp, accum_out=exp_sum[:]
+        )
+        log_sum = const.tile([P, 1], F32)
+        nc.scalar.activation(out=log_sum[:], in_=exp_sum[:], func=ACT.Ln)
+        result = const.tile([P, C], F32)
+        nc.vector.tensor_scalar(
+            out=result[:], in0=shifted[:], scalar1=log_sum[:], scalar2=None, op0=ALU.subtract
+        )
+        nc.sync.dma_start(out=out, in_=result[:])

@@ -20,6 +20,8 @@ K_PASS = P * PACK
 PASSES = K // K_PASS
 E_HALVES = E // P
 AHEAD = 2
+KEY_BANKS = [(n, g) for n in range(NETS) for g in range(PASSES)]
+HEAD_REGROUPS = 5
 
 FLOPS = 2 * NETS * B * K * E * 2 + 2 * B * NETS * E * C
 
@@ -29,8 +31,8 @@ def tile_hopfieldmodel_pa_s_kernel(tc, q_state, keys, W_lin, b_lin, out):
     with ExitStack() as ctx:
         const = ctx.enter_context(tc.tile_pool(name="const", bufs=1))
         per_net = ctx.enter_context(tc.tile_pool(name="per_net", bufs=NETS))
-        ps_t = ctx.enter_context(tc.psum_pool(name="ps_t", bufs=2))
-        ps_s = ctx.enter_context(tc.psum_pool(name="ps_s", bufs=2 * PASSES))
+        ps_t = ctx.enter_context(tc.psum_pool(name="ps_t", bufs=4))
+        ps_s = ctx.enter_context(tc.psum_pool(name="ps_s", bufs=AHEAD * PASSES))
         ctx.enter_context(tc.manual_schedule())
 
         keys_sb = [
@@ -43,9 +45,9 @@ def tile_hopfieldmodel_pa_s_kernel(tc, q_state, keys, W_lin, b_lin, out):
         def keys_view(n):
             return keys[n].rearrange("(g p j) e -> p g j e", g=PASSES, j=PACK)
 
-        nc.sync.dma_start(out=keys_sb[0][:, 0], in_=keys_view(0)[:, 0])
+        for g in range(PASSES):
+            nc.sync.dma_start(out=keys_sb[0][:, g], in_=keys_view(0)[:, g])
         nc.sync.dma_start(out=q_sb[:], in_=q_state.rearrange("n b e -> b n e"))
-        nc.sync.dma_start(out=keys_sb[0][:, 1], in_=keys_view(0)[:, 1])
         for n in range(1, NETS):
             nc.sync.dma_start(out=keys_sb[n][:], in_=keys_view(n))
         nc.sync.dma_start(
@@ -58,12 +60,16 @@ def tile_hopfieldmodel_pa_s_kernel(tc, q_state, keys, W_lin, b_lin, out):
 
         q_t = const.tile([P, NETS, B], F32)
         keys_t = [const.tile([P, PASSES, K_PASS], F32, name="keys_t%d" % n) for n in range(NETS)]
+        k_grouped = [
+            const.tile([P, PASSES, E, PACK], BF16, align_bytes=64, name="k_grouped%d" % n)
+            for n in range(NETS)
+        ]
         bank_sum = const.tile([P, NETS, PASSES], F32)
-        scores, neg_max, e_sb, e_grouped = {}, {}, {}, {}
+        scores, neg_max, e_sb, e_t, e_grouped = {}, {}, {}, {}, {}
         k_codes, k_scales, e_codes, e_scales, retrieved = {}, {}, {}, {}, {}
 
         def transpose_q():
-            qt_ps = ps_t.tile([P, NETS, B], F32, tag="et")
+            qt_ps = ps_t.tile([P, NETS, B], F32, tag="t")
             for n in range(NETS):
                 nc.tensor.transpose(
                     out=qt_ps[:, n, :], in_=q_sb[:, n, :].bitcast(F32), identity=ident[:]
@@ -71,7 +77,7 @@ def tile_hopfieldmodel_pa_s_kernel(tc, q_state, keys, W_lin, b_lin, out):
             nc.scalar.copy(out=q_t[:], in_=qt_ps[:])
 
         def transpose_keys(n, g):
-            kt_ps = ps_t.tile([P, PACK, P], F32, tag="kt")
+            kt_ps = ps_t.tile([P, PACK, P], F32, tag="t")
             for j in range(PACK):
                 nc.tensor.transpose(
                     out=kt_ps[:, j, :], in_=keys_sb[n][:, g, j, :].bitcast(F32), identity=ident[:]
@@ -100,6 +106,21 @@ def tile_hopfieldmodel_pa_s_kernel(tc, q_state, keys, W_lin, b_lin, out):
                 )
             scores[(n, g)] = s_ps
 
+        def regroup_keys(n, g):
+            nc.vector.tensor_copy(
+                out=k_grouped[n][:, g].rearrange("p (c i) j -> p c j i", i=4),
+                in_=keys_sb[n][:, g].rearrange("p j (c i) -> p c j i", i=4),
+            )
+
+        def quantise_keys(n):
+            k_codes[n] = per_net.tile([P, PASSES, E], U32, align_bytes=64, tag="k_codes", name="kc")
+            k_scales[n] = per_net.tile([P, PASSES, E], U8, align_bytes=64, tag="k_scales", name="ks")
+            nc.vector.quantize_mx(
+                out=k_codes[n][:].rearrange("p g e -> p (g e)").bitcast(FP8X4),
+                scales=k_scales[n][:].rearrange("p g e -> p (g e)"),
+                in_=k_grouped[n][:].rearrange("p g e j -> p (g e j)"),
+            )
+
         def row_max(n):
             bank_max = per_net.tile([P, PASSES], F32, tag="bank_max")
             for g in range(PASSES):
@@ -115,6 +136,8 @@ def tile_hopfieldmodel_pa_s_kernel(tc, q_state, keys, W_lin, b_lin, out):
                 op0=ALU.max,
                 op1=ALU.mult,
             )
+            if HEAD_REGROUPS + n < len(KEY_BANKS):
+                regroup_keys(*KEY_BANKS[HEAD_REGROUPS + n])
 
         def exponentiate(n):
             e_sb[n] = per_net.tile([P, PASSES, K_PASS], BF16, tag="e_sb", name="e_sb")
@@ -128,41 +151,25 @@ def tile_hopfieldmodel_pa_s_kernel(tc, q_state, keys, W_lin, b_lin, out):
                     accum_out=bank_sum[:, n, g : g + 1],
                 )
 
-        def transpose_e(n, g):
-            et_ps = ps_t.tile([P, 2, B], F32, tag="et")
-            for u in range(2):
-                nc.tensor.transpose(
-                    out=et_ps[:, u, :],
-                    in_=e_sb[n][:, g, :].bitcast(F32)[:, u * P : (u + 1) * P],
-                    identity=ident[:],
-                )
-            return et_ps
-
-        def store_e_t(n, g, et_ps):
-            if g == 0:
-                e_grouped[n] = per_net.tile(
-                    [P, PASSES, B, PACK], BF16, align_bytes=64, tag="e_grouped", name="e_grouped"
-                )
-            nc.scalar.copy(
-                out=e_grouped[n][:, g].rearrange("p b j -> p (b j)").bitcast(F32).rearrange(
-                    "p (b u) -> p b u", u=2
-                ),
-                in_=et_ps[:].rearrange("p u b -> p b u"),
-            )
-
-        def quantise_keys(n):
-            grouped = per_net.tile([P, PASSES, E, PACK], BF16, align_bytes=64, tag="k_grouped")
+        def transpose_e(n):
+            e_t[n] = ps_t.tile([P, PASSES, 2, B], F32, tag="t", name="et_ps")
             for g in range(PASSES):
-                nc.vector.tensor_copy(
-                    out=grouped[:, g].rearrange("p (c i) j -> p c j i", i=4),
-                    in_=keys_sb[n][:, g].rearrange("p j (c i) -> p c j i", i=4),
-                )
-            k_codes[n] = per_net.tile([P, PASSES, E], U32, align_bytes=64, tag="k_codes", name="kc")
-            k_scales[n] = per_net.tile([P, PASSES, E], U8, align_bytes=64, tag="k_scales", name="ks")
-            nc.vector.quantize_mx(
-                out=k_codes[n][:].rearrange("p g e -> p (g e)").bitcast(FP8X4),
-                scales=k_scales[n][:].rearrange("p g e -> p (g e)"),
-                in_=grouped[:].rearrange("p g e j -> p (g e j)"),
+                for u in range(2):
+                    nc.tensor.transpose(
+                        out=e_t[n][:, g, u, :],
+                        in_=e_sb[n][:, g, :].bitcast(F32)[:, u * P : (u + 1) * P],
+                        identity=ident[:],
+                    )
+
+        def store_e_t(n):
+            e_grouped[n] = per_net.tile(
+                [P, PASSES, B, PACK], BF16, align_bytes=64, tag="e_grouped", name="e_grouped"
+            )
+            nc.scalar.copy(
+                out=e_grouped[n][:].rearrange("p g b j -> p g (b j)").bitcast(F32).rearrange(
+                    "p g (b u) -> p g b u", u=2
+                ),
+                in_=e_t[n][:].rearrange("p g u b -> p g b u"),
             )
 
         def quantise_e(n):
@@ -190,38 +197,40 @@ def tile_hopfieldmodel_pa_s_kernel(tc, q_state, keys, W_lin, b_lin, out):
                     )
             retrieved[n] = rt_ps
 
-        store_keys_t(0, 0, transpose_keys(0, 0))
-        transpose_q()
-        store_keys_t(0, 1, transpose_keys(0, 1))
-        for g in range(PASSES):
-            score(0, g)
-            store_keys_t(1, g, transpose_keys(1, g))
-        for g in range(PASSES):
-            score(1, g)
-        quantise_keys(0)
-        row_max(0)
+        for n in range(NETS):
+            kt_banks = [transpose_keys(n, g) for g in range(PASSES)]
+            for g in range(PASSES):
+                store_keys_t(n, g, kt_banks[g])
+            if n == 0:
+                transpose_q()
+            else:
+                score(*KEY_BANKS[n - 1])
+        score(*KEY_BANKS[NETS - 1])
+        for i in range(HEAD_REGROUPS):
+            regroup_keys(*KEY_BANKS[i])
+            if i == PASSES - 1:
+                quantise_keys(0)
+        for n in range(AHEAD):
+            row_max(n)
 
         for n in range(NETS):
             exponentiate(n)
-            ahead = n + AHEAD
-            if ahead < NETS:
-                kt_banks = [transpose_keys(ahead, g) for g in range(PASSES)]
-            et_banks = [transpose_e(n, g) for g in range(PASSES)]
-            if ahead < NETS:
+            if n >= 1:
+                store_e_t(n - 1)
+            if n + AHEAD < NETS:
                 for g in range(PASSES):
-                    store_keys_t(ahead, g, kt_banks[g])
-                    score(ahead, g)
-            for g in range(PASSES):
-                store_e_t(n, g, et_banks[g])
-            if n + 1 < NETS:
-                row_max(n + 1)
-                quantise_keys(n + 1)
+                    score(n + AHEAD, g)
+                row_max(n + AHEAD)
+            transpose_e(n)
+        store_e_t(NETS - 1)
+        for n in range(1, NETS):
+            quantise_keys(n)
 
         row_sum = const.tile([P, NETS], F32)
         nc.vector.tensor_reduce(out=row_sum[:], in_=bank_sum[:], axis=AX.X, op=ALU.add)
         inv_sum = const.tile([P, NETS], F32)
         nc.vector.reciprocal(out=inv_sum[:], in_=row_sum[:])
-        spread_ps = ps_t.tile([P, NETS, B], F32, tag="kt")
+        spread_ps = ps_t.tile([P, NETS, B], F32, tag="t")
         for n in range(NETS):
             nc.tensor.transpose(
                 out=spread_ps[:, n, :],
@@ -280,21 +289,22 @@ def tile_hopfieldmodel_pa_s_kernel(tc, q_state, keys, W_lin, b_lin, out):
             )
         y = const.tile([P, C], F32)
         nc.vector.tensor_tensor(out=y[:], in0=y_ps[:], in1=bias_sb[:], op=ALU.add)
-        y_max = const.tile([P, 1], F32)
-        nc.vector.tensor_reduce(out=y_max[:], in_=y[:], axis=AX.X, op=ALU.max)
-        shifted = const.tile([P, C], F32)
-        nc.vector.tensor_scalar(
-            out=shifted[:], in0=y[:], scalar1=y_max[:], scalar2=None, op0=ALU.subtract
-        )
+        neg_y_max = const.tile([P, 1], F32)
+        nc.vector.tensor_reduce(out=neg_y_max[:], in_=y[:], axis=AX.X, op=ALU.max, negate=True)
         exp_shifted = const.tile([P, C], F32)
         exp_sum = const.tile([P, 1], F32)
         nc.scalar.activation(
-            out=exp_shifted[:], in_=shifted[:], func=ACT.Exp, accum_out=exp_sum[:]
+            out=exp_shifted[:], in_=y[:], func=ACT.Exp, bias=neg_y_max[:], accum_out=exp_sum[:]
         )
         log_sum = const.tile([P, 1], F32)
         nc.scalar.activation(out=log_sum[:], in_=exp_sum[:], func=ACT.Ln)
         result = const.tile([P, C], F32)
         nc.vector.tensor_scalar(
-            out=result[:], in0=shifted[:], scalar1=log_sum[:], scalar2=None, op0=ALU.subtract
+            out=result[:],
+            in0=y[:],
+            scalar1=neg_y_max[:],
+            scalar2=log_sum[:],
+            op0=ALU.add,
+            op1=ALU.subtract,
         )
         nc.sync.dma_start(out=out, in_=result[:])

@@ -1,3 +1,4 @@
+import math
 from contextlib import ExitStack
 
 import concourse.mybir as mybir
@@ -5,6 +6,7 @@ from concourse.masks import make_identity
 
 F32 = mybir.dt.float32
 BF16 = mybir.dt.bfloat16
+I32 = mybir.dt.int32
 U32 = mybir.dt.uint32
 U8 = mybir.dt.uint8
 FP8X4 = mybir.dt.float8_e4m3fn_x4
@@ -22,6 +24,10 @@ E_HALVES = E // P
 AHEAD = 2
 KEY_BANKS = [(n, g) for n in range(NETS) for g in range(PASSES)]
 HEAD_REGROUPS = 5
+
+LN_TERMS = 32
+EXPONENT_BITS = 0x7F800000
+SIGN_AND_EXPONENT = -(2**23)
 
 FLOPS = 2 * NETS * B * K * E * 2 + 2 * B * NETS * E * C
 
@@ -57,6 +63,11 @@ def tile_hopfieldmodel_pa_s_kernel(tc, q_state, keys, W_lin, b_lin, out):
 
         ident = const.tile([P, P], F32)
         make_identity(nc, ident[:])
+
+        ln_terms = const.tile([P, LN_TERMS + 1], F32)
+        for i in range(1, LN_TERMS + 1):
+            c = LN_TERMS - i
+            nc.gpsimd.memset(ln_terms[:, c : c + 1], 0.25**i / i)
 
         q_t = const.tile([P, NETS, B], F32)
         keys_t = [const.tile([P, PASSES, K_PASS], F32, name="keys_t%d" % n) for n in range(NETS)]
@@ -296,15 +307,48 @@ def tile_hopfieldmodel_pa_s_kernel(tc, q_state, keys, W_lin, b_lin, out):
         nc.scalar.activation(
             out=exp_shifted[:], in_=y[:], func=ACT.Exp, bias=neg_y_max[:], accum_out=exp_sum[:]
         )
-        log_sum = const.tile([P, 1], F32)
-        nc.scalar.activation(out=log_sum[:], in_=exp_sum[:], func=ACT.Ln)
+        flipped = const.tile([P, 1], I32)
+        nc.vector.tensor_scalar(
+            out=flipped[:],
+            in0=exp_sum[:].bitcast(I32),
+            scalar1=EXPONENT_BITS,
+            scalar2=SIGN_AND_EXPONENT,
+            op0=ALU.bitwise_and,
+            op1=ALU.bitwise_xor,
+        )
+        u4 = const.tile([P, 1], F32)
+        nc.vector.tensor_scalar(
+            out=u4[:],
+            in0=exp_sum[:],
+            scalar1=flipped[:].bitcast(F32),
+            scalar2=4.0,
+            op0=ALU.mult,
+            op1=ALU.add,
+        )
+        nc.vector.tensor_scalar(
+            out=ln_terms[:, LN_TERMS : LN_TERMS + 1],
+            in0=flipped[:],
+            scalar1=float(2**31 - 129 * 2**23),
+            scalar2=math.log(2.0) / 2**23,
+            op0=ALU.add,
+            op1=ALU.mult,
+        )
+        neg_log = const.tile([P, LN_TERMS + 1], F32)
+        nc.vector.tensor_tensor_scan(
+            out=neg_log[:],
+            data0=u4[:].to_broadcast([P, LN_TERMS + 1]),
+            data1=ln_terms[:],
+            initial=0.0,
+            op0=ALU.mult,
+            op1=ALU.add,
+        )
         result = const.tile([P, C], F32)
         nc.vector.tensor_scalar(
             out=result[:],
             in0=y[:],
             scalar1=neg_y_max[:],
-            scalar2=log_sum[:],
+            scalar2=neg_log[:, LN_TERMS : LN_TERMS + 1],
             op0=ALU.add,
-            op1=ALU.subtract,
+            op1=ALU.add,
         )
         nc.sync.dma_start(out=out, in_=result[:])

@@ -21,9 +21,7 @@ PACK = 4
 K_PASS = P * PACK
 PASSES = K // K_PASS
 E_HALVES = E // P
-AHEAD = 2
-KEY_BANKS = [(n, g) for n in range(NETS) for g in range(PASSES)]
-HEAD_REGROUPS = 5
+PAIR = 2
 
 LN_TERMS = 32
 EXPONENT_BITS = 0x7F800000
@@ -38,7 +36,7 @@ def tile_hopfieldmodel_pa_s_kernel(tc, q_state, keys, W_lin, b_lin, out):
         const = ctx.enter_context(tc.tile_pool(name="const", bufs=1))
         per_net = ctx.enter_context(tc.tile_pool(name="per_net", bufs=NETS))
         ps_t = ctx.enter_context(tc.psum_pool(name="ps_t", bufs=4))
-        ps_s = ctx.enter_context(tc.psum_pool(name="ps_s", bufs=AHEAD * PASSES))
+        ps_s = ctx.enter_context(tc.psum_pool(name="ps_s", bufs=4))
         ctx.enter_context(tc.manual_schedule())
 
         keys_sb = [
@@ -76,8 +74,29 @@ def tile_hopfieldmodel_pa_s_kernel(tc, q_state, keys, W_lin, b_lin, out):
             for n in range(NETS)
         ]
         bank_sum = const.tile([P, NETS, PASSES], F32)
-        scores, neg_max, e_sb, e_t, e_grouped = {}, {}, {}, {}, {}
+        bank_max = const.tile([P, NETS, PASSES], F32)
+        neg_max = const.tile([P, NETS], F32)
+        row_sum = const.tile([P, NETS], F32)
+        inv_sum = const.tile([P, NETS], F32)
+        inv_spread = const.tile([P, NETS, B], F32)
+        w_grouped = const.tile([P, PASSES, C, PACK], BF16, align_bytes=64)
+        w_codes = const.tile([P, PASSES, C], U32, align_bytes=64)
+        w_scales = const.tile([P, PASSES, C], U8, align_bytes=64)
+        h_grouped = const.tile([P, PASSES, B, PACK], BF16, align_bytes=64)
+        h_codes = const.tile([P, PASSES, B], U32, align_bytes=64)
+        h_scales = const.tile([P, PASSES, B], U8, align_bytes=64)
+        kt_ps, scores, e_sb, e_t, e_grouped, spread_ps = {}, {}, {}, {}, {}, {}
         k_codes, k_scales, e_codes, e_scales, retrieved = {}, {}, {}, {}, {}
+
+        def copy_on(engine, out, in_):
+            if engine == "scalar":
+                nc.scalar.copy(out=out, in_=in_)
+            elif engine == "vector":
+                nc.vector.tensor_copy(out=out, in_=in_)
+            else:
+                nc.gpsimd.tensor_scalar(
+                    out=out, in0=in_, scalar1=1.0, scalar2=0.0, op0=ALU.mult, op1=ALU.add
+                )
 
         def transpose_q():
             qt_ps = ps_t.tile([P, NETS, B], F32, tag="t")
@@ -85,20 +104,24 @@ def tile_hopfieldmodel_pa_s_kernel(tc, q_state, keys, W_lin, b_lin, out):
                 nc.tensor.transpose(
                     out=qt_ps[:, n, :], in_=q_sb[:, n, :].bitcast(F32), identity=ident[:]
                 )
-            nc.scalar.copy(out=q_t[:], in_=qt_ps[:])
+            kt_ps["q"] = qt_ps
+
+        def store_q_t(engine):
+            copy_on(engine, q_t[:], kt_ps["q"][:])
 
         def transpose_keys(n, g):
-            kt_ps = ps_t.tile([P, PACK, P], F32, tag="t")
+            ps = ps_t.tile([P, PACK, P], F32, tag="t")
             for j in range(PACK):
                 nc.tensor.transpose(
-                    out=kt_ps[:, j, :], in_=keys_sb[n][:, g, j, :].bitcast(F32), identity=ident[:]
+                    out=ps[:, j, :], in_=keys_sb[n][:, g, j, :].bitcast(F32), identity=ident[:]
                 )
-            return kt_ps
+            kt_ps[(n, g)] = ps
 
-        def store_keys_t(n, g, kt_ps):
-            nc.scalar.copy(
-                out=keys_t[n][:, g, :].rearrange("w (u p i) -> w u p i", u=2, i=2),
-                in_=kt_ps[:].rearrange("w (u i) p -> w u p i", i=2),
+        def store_keys_t(n, g, engine):
+            copy_on(
+                engine,
+                keys_t[n][:, g, :].rearrange("w (u p i) -> w u p i", u=2, i=2),
+                kt_ps[(n, g)][:].rearrange("w (u i) p -> w u p i", i=2),
             )
 
         def score(n, g):
@@ -117,11 +140,15 @@ def tile_hopfieldmodel_pa_s_kernel(tc, q_state, keys, W_lin, b_lin, out):
                 )
             scores[(n, g)] = s_ps
 
-        def regroup_keys(n, g):
-            nc.vector.tensor_copy(
-                out=k_grouped[n][:, g].rearrange("p (c i) j -> p c j i", i=4),
-                in_=keys_sb[n][:, g].rearrange("p j (c i) -> p c j i", i=4),
-            )
+        def regroup_keys(n, g, engine):
+            if engine == "vector":
+                copy_on(
+                    engine,
+                    k_grouped[n][:, g].rearrange("p (c i) j -> p c j i", i=4),
+                    keys_sb[n][:, g].rearrange("p j (c i) -> p c j i", i=4),
+                )
+            else:
+                copy_on(engine, k_grouped[n][:, g], keys_sb[n][:, g].rearrange("p j e -> p e j"))
 
         def quantise_keys(n):
             k_codes[n] = per_net.tile([P, PASSES, E], U32, align_bytes=64, tag="k_codes", name="kc")
@@ -132,35 +159,31 @@ def tile_hopfieldmodel_pa_s_kernel(tc, q_state, keys, W_lin, b_lin, out):
                 in_=k_grouped[n][:].rearrange("p g e j -> p (g e j)"),
             )
 
-        def row_max(n):
-            bank_max = per_net.tile([P, PASSES], F32, tag="bank_max")
-            for g in range(PASSES):
-                nc.vector.tensor_reduce(
-                    out=bank_max[:, g : g + 1], in_=scores[(n, g)][:], axis=AX.X, op=ALU.max
-                )
-            neg_max[n] = per_net.tile([P, 1], F32, tag="neg_max", name="neg_max")
+        def bank_maximum(n, g):
+            nc.vector.tensor_reduce(
+                out=bank_max[:, n, g : g + 1], in_=scores[(n, g)][:], axis=AX.X, op=ALU.max
+            )
+
+        def row_maximum(n):
             nc.vector.tensor_scalar(
-                out=neg_max[n][:],
-                in0=bank_max[:, 0:1],
-                scalar1=bank_max[:, 1:2],
+                out=neg_max[:, n : n + 1],
+                in0=bank_max[:, n, 0:1],
+                scalar1=bank_max[:, n, 1:2],
                 scalar2=-BETA,
                 op0=ALU.max,
                 op1=ALU.mult,
             )
-            if HEAD_REGROUPS + n < len(KEY_BANKS):
-                regroup_keys(*KEY_BANKS[HEAD_REGROUPS + n])
-
-        def exponentiate(n):
             e_sb[n] = per_net.tile([P, PASSES, K_PASS], BF16, tag="e_sb", name="e_sb")
-            for g in range(PASSES):
-                nc.scalar.activation(
-                    out=e_sb[n][:, g, :],
-                    in_=scores[(n, g)][:],
-                    func=ACT.Exp,
-                    bias=neg_max[n][:],
-                    scale=BETA,
-                    accum_out=bank_sum[:, n, g : g + 1],
-                )
+
+        def exponentiate(n, g):
+            nc.scalar.activation(
+                out=e_sb[n][:, g, :],
+                in_=scores[(n, g)][:],
+                func=ACT.Exp,
+                bias=neg_max[:, n : n + 1],
+                scale=BETA,
+                accum_out=bank_sum[:, n, g : g + 1],
+            )
 
         def transpose_e(n):
             e_t[n] = ps_t.tile([P, PASSES, 2, B], F32, tag="t", name="et_ps")
@@ -172,15 +195,16 @@ def tile_hopfieldmodel_pa_s_kernel(tc, q_state, keys, W_lin, b_lin, out):
                         identity=ident[:],
                     )
 
-        def store_e_t(n):
+        def store_e_t(n, engine):
             e_grouped[n] = per_net.tile(
                 [P, PASSES, B, PACK], BF16, align_bytes=64, tag="e_grouped", name="e_grouped"
             )
-            nc.scalar.copy(
-                out=e_grouped[n][:].rearrange("p g b j -> p g (b j)").bitcast(F32).rearrange(
+            copy_on(
+                engine,
+                e_grouped[n][:].rearrange("p g b j -> p g (b j)").bitcast(F32).rearrange(
                     "p g (b u) -> p g b u", u=2
                 ),
-                in_=e_t[n][:].rearrange("p g u b -> p g b u"),
+                e_t[n][:].rearrange("p g u b -> p g b u"),
             )
 
         def quantise_e(n):
@@ -208,68 +232,36 @@ def tile_hopfieldmodel_pa_s_kernel(tc, q_state, keys, W_lin, b_lin, out):
                     )
             retrieved[n] = rt_ps
 
-        for n in range(NETS):
-            kt_banks = [transpose_keys(n, g) for g in range(PASSES)]
-            for g in range(PASSES):
-                store_keys_t(n, g, kt_banks[g])
-            if n == 0:
-                transpose_q()
-            else:
-                score(*KEY_BANKS[n - 1])
-        score(*KEY_BANKS[NETS - 1])
-        for i in range(HEAD_REGROUPS):
-            regroup_keys(*KEY_BANKS[i])
-            if i == PASSES - 1:
-                quantise_keys(0)
-        for n in range(AHEAD):
-            row_max(n)
-
-        for n in range(NETS):
-            exponentiate(n)
-            if n >= 1:
-                store_e_t(n - 1)
-            if n + AHEAD < NETS:
-                for g in range(PASSES):
-                    score(n + AHEAD, g)
-                row_max(n + AHEAD)
-            transpose_e(n)
-        store_e_t(NETS - 1)
-        for n in range(1, NETS):
-            quantise_keys(n)
-
-        row_sum = const.tile([P, NETS], F32)
-        nc.vector.tensor_reduce(out=row_sum[:], in_=bank_sum[:], axis=AX.X, op=ALU.add)
-        inv_sum = const.tile([P, NETS], F32)
-        nc.vector.reciprocal(out=inv_sum[:], in_=row_sum[:])
-        spread_ps = ps_t.tile([P, NETS, B], F32, tag="t")
-        for n in range(NETS):
-            nc.tensor.transpose(
-                out=spread_ps[:, n, :],
-                in_=inv_sum[:, n : n + 1].to_broadcast([P, P]),
-                identity=ident[:],
+        def invert_sums(first):
+            pair = slice(first, first + PAIR)
+            nc.vector.tensor_reduce(
+                out=row_sum[:, pair], in_=bank_sum[:, pair, :], axis=AX.X, op=ALU.add
             )
-        inv_spread = const.tile([P, NETS, B], F32)
-        nc.scalar.copy(out=inv_spread[:], in_=spread_ps[:])
+            nc.vector.reciprocal(out=inv_sum[:, pair], in_=row_sum[:, pair])
 
-        w_grouped = const.tile([P, PASSES, C, PACK], BF16, align_bytes=64)
-        nc.scalar.copy(out=w_grouped[:], in_=w_sb[:].rearrange("p g t c -> p g c t"))
-        w_codes = const.tile([P, PASSES, C], U32, align_bytes=64)
-        w_scales = const.tile([P, PASSES, C], U8, align_bytes=64)
-
-        for n in range(NETS):
-            quantise_e(n)
-            retrieve(n)
-
-        h_grouped = const.tile([P, PASSES, B, PACK], BF16, align_bytes=64)
-        h_codes = const.tile([P, PASSES, B], U32, align_bytes=64)
-        h_scales = const.tile([P, PASSES, B], U8, align_bytes=64)
-        for n in range(NETS):
-            if n == NETS - 1:
-                nc.vector.quantize_mx(
-                    out=w_codes[:].rearrange("p g c -> p (g c)").bitcast(FP8X4),
-                    scales=w_scales[:].rearrange("p g c -> p (g c)"),
-                    in_=w_grouped[:].rearrange("p g c t -> p (g c t)"),
+        def spread_inverses(first):
+            spread_ps[first] = ps_t.tile([P, PAIR, B], F32, tag="t", name="spread_ps")
+            for i in range(PAIR):
+                nc.tensor.transpose(
+                    out=spread_ps[first][:, i, :],
+                    in_=inv_sum[:, first + i : first + i + 1].to_broadcast([P, P]),
+                    identity=ident[:],
                 )
+
+        def store_spread(first, engine):
+            copy_on(engine, inv_spread[:, first : first + PAIR, :], spread_ps[first][:])
+
+        def regroup_w(engine):
+            copy_on(engine, w_grouped[:], w_sb[:].rearrange("p g t c -> p g c t"))
+
+        def quantise_w():
+            nc.vector.quantize_mx(
+                out=w_codes[:].rearrange("p g c -> p (g c)").bitcast(FP8X4),
+                scales=w_scales[:].rearrange("p g c -> p (g c)"),
+                in_=w_grouped[:].rearrange("p g c t -> p (g c t)"),
+            )
+
+        def hidden(n):
             t0 = E_HALVES * (n % 2)
             nc.vector.scalar_tensor_tensor(
                 out=h_grouped[:, n // 2, :, t0 : t0 + E_HALVES],
@@ -279,13 +271,102 @@ def tile_hopfieldmodel_pa_s_kernel(tc, q_state, keys, W_lin, b_lin, out):
                 op0=ALU.max,
                 op1=ALU.mult,
             )
-            if n % 2 == 1:
-                g = n // 2
-                nc.vector.quantize_mx(
-                    out=h_codes[:, g, :].bitcast(FP8X4),
-                    scales=h_scales[:, g, :],
-                    in_=h_grouped[:, g].rearrange("p b t -> p (b t)"),
-                )
+
+        def quantise_hidden(g):
+            nc.vector.quantize_mx(
+                out=h_codes[:, g, :].bitcast(FP8X4),
+                scales=h_scales[:, g, :],
+                in_=h_grouped[:, g].rearrange("p b t -> p (b t)"),
+            )
+
+        regroup_keys(0, 0, "vector")
+        transpose_keys(0, 0)
+        transpose_keys(0, 1)
+        regroup_keys(0, 1, "vector")
+        store_keys_t(0, 0, "scalar")
+        transpose_q()
+        quantise_keys(0)
+        store_keys_t(0, 1, "scalar")
+        store_q_t("scalar")
+        regroup_keys(1, 0, "vector")
+        transpose_keys(1, 0)
+        transpose_keys(1, 1)
+        regroup_keys(1, 1, "vector")
+        store_keys_t(1, 0, "scalar")
+        score(0, 0)
+        regroup_keys(2, 0, "gpsimd")
+        quantise_keys(1)
+        store_keys_t(1, 1, "scalar")
+        transpose_keys(2, 0)
+        score(0, 1)
+        bank_maximum(0, 0)
+        store_keys_t(2, 0, "scalar")
+        transpose_keys(2, 1)
+        regroup_keys(2, 1, "gpsimd")
+        bank_maximum(0, 1)
+        transpose_keys(3, 0)
+        store_keys_t(2, 1, "scalar")
+        score(1, 0)
+        row_maximum(0)
+        store_keys_t(3, 0, "vector")
+        exponentiate(0, 0)
+        transpose_keys(3, 1)
+        regroup_keys(3, 0, "gpsimd")
+        bank_maximum(1, 0)
+        score(1, 1)
+        exponentiate(0, 1)
+        score(2, 0)
+        store_keys_t(3, 1, "scalar")
+        bank_maximum(1, 1)
+        regroup_keys(3, 1, "gpsimd")
+        score(2, 1)
+        row_maximum(1)
+        quantise_keys(2)
+        transpose_e(0)
+        exponentiate(1, 0)
+        bank_maximum(2, 0)
+        regroup_w("gpsimd")
+        exponentiate(1, 1)
+        score(3, 0)
+        bank_maximum(2, 1)
+        store_e_t(0, "scalar")
+        score(3, 1)
+        row_maximum(2)
+        invert_sums(0)
+        transpose_e(1)
+        exponentiate(2, 0)
+        quantise_e(0)
+        spread_inverses(0)
+        bank_maximum(3, 0)
+        exponentiate(2, 1)
+        retrieve(0)
+        bank_maximum(3, 1)
+        store_e_t(1, "scalar")
+        transpose_e(2)
+        row_maximum(3)
+        store_spread(0, "scalar")
+        quantise_e(1)
+        exponentiate(3, 0)
+        hidden(0)
+        retrieve(1)
+        quantise_keys(3)
+        exponentiate(3, 1)
+        store_e_t(2, "scalar")
+        transpose_e(3)
+        invert_sums(2)
+        hidden(1)
+        spread_inverses(2)
+        quantise_e(2)
+        store_e_t(3, "scalar")
+        quantise_w()
+        retrieve(2)
+        store_spread(2, "scalar")
+        quantise_e(3)
+        quantise_hidden(0)
+        retrieve(3)
+        hidden(2)
+        hidden(3)
+        quantise_hidden(1)
 
         y_ps = ps_s.tile([P, C], F32, tag="s")
         for g in range(PASSES):

@@ -74,8 +74,9 @@ def tile_hopfieldmodel_pa_s_kernel(tc, q_state, keys, W_lin, b_lin, out):
             for n in range(NETS)
         ]
         bank_sum = const.tile([P, NETS, PASSES], F32)
-        bank_max = const.tile([P, NETS, PASSES], F32)
-        neg_max = const.tile([P, NETS], F32)
+        neg_max = const.tile([P, NETS, PASSES], F32)
+        scaled_scores = const.tile([P, K_PASS], BF16)
+        e_sb = [const.tile([P, PASSES, K_PASS], BF16, name="e_sb%d" % n) for n in range(NETS)]
         row_sum = const.tile([P, NETS], F32)
         inv_sum = const.tile([P, NETS], F32)
         inv_spread = const.tile([P, NETS, B], F32)
@@ -85,7 +86,7 @@ def tile_hopfieldmodel_pa_s_kernel(tc, q_state, keys, W_lin, b_lin, out):
         h_grouped = const.tile([P, PASSES, B, PACK], BF16, align_bytes=64)
         h_codes = const.tile([P, PASSES, B], U32, align_bytes=64)
         h_scales = const.tile([P, PASSES, B], U8, align_bytes=64)
-        kt_ps, scores, e_sb, e_t, e_grouped, spread_ps = {}, {}, {}, {}, {}, {}
+        kt_ps, scores, e_t, e_grouped, spread_ps = {}, {}, {}, {}, {}
         k_codes, k_scales, e_codes, e_scales, retrieved = {}, {}, {}, {}, {}
 
         def copy_on(engine, out, in_):
@@ -160,27 +161,22 @@ def tile_hopfieldmodel_pa_s_kernel(tc, q_state, keys, W_lin, b_lin, out):
             )
 
         def bank_maximum(n, g):
-            nc.vector.tensor_reduce(
-                out=bank_max[:, n, g : g + 1], in_=scores[(n, g)][:], axis=AX.X, op=ALU.max
-            )
-
-        def row_maximum(n):
             nc.vector.tensor_scalar(
-                out=neg_max[:, n : n + 1],
-                in0=bank_max[:, n, 0:1],
-                scalar1=bank_max[:, n, 1:2],
-                scalar2=-BETA,
-                op0=ALU.max,
-                op1=ALU.mult,
+                out=scaled_scores[:],
+                in0=scores[(n, g)][:],
+                scalar1=-BETA,
+                scalar2=None if g == 0 else neg_max[:, n, g - 1 : g],
+                op0=ALU.mult,
+                op1=ALU.min,
+                accum_out=neg_max[:, n, g : g + 1],
             )
-            e_sb[n] = per_net.tile([P, PASSES, K_PASS], BF16, tag="e_sb", name="e_sb")
 
         def exponentiate(n, g):
             nc.scalar.activation(
                 out=e_sb[n][:, g, :],
                 in_=scores[(n, g)][:],
                 func=ACT.Exp,
-                bias=neg_max[:, n : n + 1],
+                bias=neg_max[:, n, PASSES - 1 : PASSES],
                 scale=BETA,
                 accum_out=bank_sum[:, n, g : g + 1],
             )
@@ -285,8 +281,8 @@ def tile_hopfieldmodel_pa_s_kernel(tc, q_state, keys, W_lin, b_lin, out):
         regroup_keys(0, 1, "vector")
         store_keys_t(0, 0, "scalar")
         transpose_q()
-        quantise_keys(0)
         store_keys_t(0, 1, "scalar")
+        quantise_keys(0)
         store_q_t("scalar")
         regroup_keys(1, 0, "vector")
         transpose_keys(1, 0)
@@ -294,75 +290,71 @@ def tile_hopfieldmodel_pa_s_kernel(tc, q_state, keys, W_lin, b_lin, out):
         regroup_keys(1, 1, "vector")
         store_keys_t(1, 0, "scalar")
         score(0, 0)
-        regroup_keys(2, 0, "gpsimd")
-        quantise_keys(1)
         store_keys_t(1, 1, "scalar")
+        quantise_keys(1)
         transpose_keys(2, 0)
         score(0, 1)
-        bank_maximum(0, 0)
         store_keys_t(2, 0, "scalar")
+        regroup_keys(2, 0, "vector")
         transpose_keys(2, 1)
-        regroup_keys(2, 1, "gpsimd")
-        bank_maximum(0, 1)
+        bank_maximum(0, 0)
+        regroup_keys(3, 0, "gpsimd")
         transpose_keys(3, 0)
         store_keys_t(2, 1, "scalar")
         score(1, 0)
-        row_maximum(0)
+        bank_maximum(0, 1)
+        transpose_keys(3, 1)
+        score(1, 1)
+        regroup_keys(3, 1, "gpsimd")
         store_keys_t(3, 0, "vector")
         exponentiate(0, 0)
-        transpose_keys(3, 1)
-        regroup_keys(3, 0, "gpsimd")
         bank_maximum(1, 0)
-        score(1, 1)
         exponentiate(0, 1)
         score(2, 0)
-        store_keys_t(3, 1, "scalar")
         bank_maximum(1, 1)
-        regroup_keys(3, 1, "gpsimd")
+        regroup_keys(2, 1, "gpsimd")
+        store_keys_t(3, 1, "scalar")
         score(2, 1)
-        row_maximum(1)
-        quantise_keys(2)
+        bank_maximum(2, 0)
         transpose_e(0)
         exponentiate(1, 0)
-        bank_maximum(2, 0)
-        regroup_w("gpsimd")
+        bank_maximum(2, 1)
         exponentiate(1, 1)
         score(3, 0)
-        bank_maximum(2, 1)
+        quantise_keys(2)
         store_e_t(0, "scalar")
         score(3, 1)
-        row_maximum(2)
-        invert_sums(0)
-        transpose_e(1)
         exponentiate(2, 0)
+        transpose_e(1)
         quantise_e(0)
-        spread_inverses(0)
-        bank_maximum(3, 0)
+        invert_sums(0)
         exponentiate(2, 1)
+        bank_maximum(3, 0)
+        spread_inverses(0)
         retrieve(0)
-        bank_maximum(3, 1)
         store_e_t(1, "scalar")
+        bank_maximum(3, 1)
         transpose_e(2)
-        row_maximum(3)
         store_spread(0, "scalar")
-        quantise_e(1)
+        regroup_w("vector")
         exponentiate(3, 0)
-        hidden(0)
-        retrieve(1)
-        quantise_keys(3)
+        quantise_e(1)
         exponentiate(3, 1)
+        quantise_keys(3)
+        retrieve(1)
         store_e_t(2, "scalar")
         transpose_e(3)
+        hidden(0)
         invert_sums(2)
         hidden(1)
+        store_e_t(3, "scalar")
         spread_inverses(2)
         quantise_e(2)
-        store_e_t(3, "scalar")
-        quantise_w()
-        retrieve(2)
         store_spread(2, "scalar")
-        quantise_e(3)
         quantise_hidden(0)
+        retrieve(2)
+        quantise_e(3)
+        quantise_w()
         retrieve(3)
         hidden(2)
         hidden(3)

@@ -79,7 +79,7 @@ def tile_hopfieldmodel_pa_s_kernel(tc, q_state, keys, W_lin, b_lin, out):
         e_sb = [const.tile([P, PASSES, K_PASS], BF16, name="e_sb%d" % n) for n in range(NETS)]
         row_sum = const.tile([P, NETS], F32)
         inv_sum = const.tile([P, NETS], F32)
-        inv_spread = const.tile([P, NETS, B], F32)
+        inv_spread = {n: const.tile([P, B, PAIR], F32, name="inv_spread%d" % n) for n in range(0, NETS, PAIR)}
         w_grouped = const.tile([P, PASSES, C, PACK], BF16, align_bytes=64)
         w_codes = const.tile([P, PASSES, C], U32, align_bytes=64)
         w_scales = const.tile([P, PASSES, C], U8, align_bytes=64)
@@ -213,12 +213,14 @@ def tile_hopfieldmodel_pa_s_kernel(tc, q_state, keys, W_lin, b_lin, out):
             )
 
         def retrieve(n):
-            rt_ps = ps_s.tile([P, E_HALVES, B], F32, tag="s")
+            if n % PAIR == 0:
+                retrieved[n] = ps_s.tile([P, PAIR, E_HALVES, B], F32, tag="s", name="rt_ps")
+            rt_ps = retrieved[n - n % PAIR]
             for half in range(E_HALVES):
                 cols = slice(half * P, (half + 1) * P)
                 for g in range(PASSES):
                     nc.tensor.matmul_mx(
-                        out=rt_ps[:, half, :],
+                        out=rt_ps[:, n % PAIR, half, :],
                         lhsT=k_codes[n][:, g, cols].bitcast(FP8X4),
                         lhsT_scale=k_scales[n][:, g, cols],
                         rhs=e_codes[n][:, g, :].bitcast(FP8X4),
@@ -226,7 +228,6 @@ def tile_hopfieldmodel_pa_s_kernel(tc, q_state, keys, W_lin, b_lin, out):
                         start=(g == 0),
                         stop=(g == PASSES - 1),
                     )
-            retrieved[n] = rt_ps
 
         def invert_sums(first):
             pair = slice(first, first + PAIR)
@@ -245,7 +246,9 @@ def tile_hopfieldmodel_pa_s_kernel(tc, q_state, keys, W_lin, b_lin, out):
                 )
 
         def store_spread(first, engine):
-            copy_on(engine, inv_spread[:, first : first + PAIR, :], spread_ps[first][:])
+            copy_on(
+                engine, inv_spread[first][:], spread_ps[first][:].rearrange("p n b -> p b n")
+            )
 
         def regroup_w(engine):
             copy_on(engine, w_grouped[:], w_sb[:].rearrange("p g t c -> p g c t"))
@@ -257,13 +260,12 @@ def tile_hopfieldmodel_pa_s_kernel(tc, q_state, keys, W_lin, b_lin, out):
                 in_=w_grouped[:].rearrange("p g c t -> p (g c t)"),
             )
 
-        def hidden(n):
-            t0 = E_HALVES * (n % 2)
+        def hidden_pair(first):
             nc.vector.scalar_tensor_tensor(
-                out=h_grouped[:, n // 2, :, t0 : t0 + E_HALVES],
-                in0=retrieved[n][:].rearrange("p t b -> p b t"),
+                out=h_grouped[:, first // PAIR].rearrange("p b (i t) -> p b i t", i=PAIR),
+                in0=retrieved[first][:].rearrange("p i t b -> p b i t"),
                 scalar=0.0,
-                in1=inv_spread[:, n, :].unsqueeze(2).to_broadcast([P, B, E_HALVES]),
+                in1=inv_spread[first][:].unsqueeze(3).to_broadcast([P, B, PAIR, E_HALVES]),
                 op0=ALU.max,
                 op1=ALU.mult,
             )
@@ -344,20 +346,18 @@ def tile_hopfieldmodel_pa_s_kernel(tc, q_state, keys, W_lin, b_lin, out):
         retrieve(1)
         store_e_t(2, "scalar")
         transpose_e(3)
-        hidden(0)
         invert_sums(2)
-        hidden(1)
-        store_e_t(3, "scalar")
+        hidden_pair(0)
         spread_inverses(2)
+        store_e_t(3, "scalar")
         quantise_e(2)
-        store_spread(2, "scalar")
         quantise_hidden(0)
+        store_spread(2, "scalar")
         retrieve(2)
         quantise_e(3)
         quantise_w()
         retrieve(3)
-        hidden(2)
-        hidden(3)
+        hidden_pair(2)
         quantise_hidden(1)
 
         y_ps = ps_s.tile([P, C], F32, tag="s")

@@ -23,7 +23,7 @@ PASSES = K // K_PASS
 E_HALVES = E // P
 PAIR = 2
 
-LN_TERMS = 32
+LN_TERMS = 26
 EXPONENT_BITS = 0x7F800000
 SIGN_AND_EXPONENT = -(2**23)
 
@@ -59,13 +59,37 @@ def tile_hopfieldmodel_pa_s_kernel(tc, q_state, keys, W_lin, b_lin, out):
         )
         nc.sync.dma_start(out=bias_sb[:], in_=b_lin.partition_broadcast(P))
 
+        zeros = const.tile([P, P], F32)
+        nc.vector.memset(zeros[:], 0.0)
         ident = const.tile([P, P], F32)
         make_identity(nc, ident[:])
 
         ln_terms = const.tile([P, LN_TERMS + 1], F32)
         for i in range(1, LN_TERMS + 1):
             c = LN_TERMS - i
-            nc.gpsimd.memset(ln_terms[:, c : c + 1], 0.25**i / i)
+            nc.vector.memset(ln_terms[:, c : c + 1], 0.25**i / i)
+
+        warm_ps = {}
+
+        def warm_plain():
+            if "plain" not in warm_ps:
+                warm_ps["plain"] = ps_s.tile([P, P], F32, tag="s", name="warm_plain_ps")
+            nc.tensor.matmul(
+                out=warm_ps["plain"][:], lhsT=zeros[:], rhs=zeros[:], start=True, stop=True
+            )
+
+        def warm_mx():
+            if "mx" not in warm_ps:
+                warm_ps["mx"] = ps_s.tile([P, PASSES * E], F32, tag="s", name="warm_mx_ps")
+            nc.tensor.matmul_mx(
+                out=warm_ps["mx"][:],
+                lhsT=k_codes[0][:, 0, :P].bitcast(FP8X4),
+                lhsT_scale=k_scales[0][:, 0, :P],
+                rhs=k_codes[0][:].rearrange("p g e -> p (g e)").bitcast(FP8X4),
+                rhs_scale=k_scales[0][:].rearrange("p g e -> p (g e)"),
+                start=True,
+                stop=True,
+            )
 
         q_t = const.tile([P, NETS, B], F32)
         keys_t = [const.tile([P, PASSES, K_PASS], F32, name="keys_t%d" % n) for n in range(NETS)]
@@ -277,39 +301,47 @@ def tile_hopfieldmodel_pa_s_kernel(tc, q_state, keys, W_lin, b_lin, out):
                 in_=h_grouped[:, g].rearrange("p b t -> p (b t)"),
             )
 
+        warm_plain()
+        warm_plain()
+        warm_plain()
+        warm_plain()
         regroup_keys(0, 0, "vector")
         transpose_keys(0, 0)
-        transpose_keys(0, 1)
+        warm_plain()
         regroup_keys(0, 1, "vector")
         store_keys_t(0, 0, "scalar")
-        transpose_q()
-        store_keys_t(0, 1, "scalar")
+        transpose_keys(0, 1)
+        warm_plain()
         quantise_keys(0)
+        store_keys_t(0, 1, "scalar")
+        transpose_q()
+        warm_plain()
         store_q_t("scalar")
         regroup_keys(1, 0, "vector")
         transpose_keys(1, 0)
-        transpose_keys(1, 1)
+        warm_plain()
         regroup_keys(1, 1, "vector")
         store_keys_t(1, 0, "scalar")
+        transpose_keys(1, 1)
         score(0, 0)
-        store_keys_t(1, 1, "scalar")
         quantise_keys(1)
+        store_keys_t(1, 1, "scalar")
         transpose_keys(2, 0)
+        regroup_keys(2, 0, "vector")
         score(0, 1)
         store_keys_t(2, 0, "scalar")
-        regroup_keys(2, 0, "vector")
         transpose_keys(2, 1)
         bank_maximum(0, 0)
         regroup_keys(3, 0, "gpsimd")
         transpose_keys(3, 0)
         store_keys_t(2, 1, "scalar")
-        score(1, 0)
         bank_maximum(0, 1)
+        score(1, 0)
         transpose_keys(3, 1)
-        score(1, 1)
         regroup_keys(3, 1, "gpsimd")
         store_keys_t(3, 0, "vector")
         exponentiate(0, 0)
+        score(1, 1)
         bank_maximum(1, 0)
         exponentiate(0, 1)
         score(2, 0)
@@ -336,28 +368,36 @@ def tile_hopfieldmodel_pa_s_kernel(tc, q_state, keys, W_lin, b_lin, out):
         retrieve(0)
         store_e_t(1, "scalar")
         bank_maximum(3, 1)
+        warm_mx()
         transpose_e(2)
         store_spread(0, "scalar")
         regroup_w("vector")
+        warm_mx()
         exponentiate(3, 0)
         quantise_e(1)
         exponentiate(3, 1)
         quantise_keys(3)
         retrieve(1)
         store_e_t(2, "scalar")
-        transpose_e(3)
+        warm_mx()
         invert_sums(2)
         hidden_pair(0)
-        spread_inverses(2)
-        store_e_t(3, "scalar")
+        warm_mx()
+        transpose_e(3)
         quantise_e(2)
+        warm_mx()
         quantise_hidden(0)
-        store_spread(2, "scalar")
+        store_e_t(3, "scalar")
+        spread_inverses(2)
+        warm_mx()
         retrieve(2)
+        store_spread(2, "scalar")
         quantise_e(3)
         quantise_w()
         retrieve(3)
+        warm_mx()
         hidden_pair(2)
+        warm_mx()
         quantise_hidden(1)
 
         y_ps = ps_s.tile([P, C], F32, tag="s")

@@ -49,11 +49,12 @@ def tile_hopfieldmodel_pa_s_kernel(tc, q_state, keys, W_lin, b_lin, out):
         def keys_view(n):
             return keys[n].rearrange("(g p j) e -> p g j e", g=PASSES, j=PACK)
 
-        for g in range(PASSES):
-            nc.sync.dma_start(out=keys_sb[0][:, g], in_=keys_view(0)[:, g])
+        nc.sync.dma_start(out=keys_sb[0][:, 0], in_=keys_view(0)[:, 0])
         nc.sync.dma_start(out=q_sb[:], in_=q_state.rearrange("n b e -> b n e"))
+        nc.sync.dma_start(out=keys_sb[0][:, 1], in_=keys_view(0)[:, 1])
         for n in range(1, NETS):
-            nc.sync.dma_start(out=keys_sb[n][:], in_=keys_view(n))
+            for g in range(PASSES):
+                nc.sync.dma_start(out=keys_sb[n][:, g], in_=keys_view(n)[:, g])
         nc.sync.dma_start(
             out=w_sb[:], in_=W_lin.rearrange("(g t p) c -> p g t c", g=PASSES, t=PACK)
         )
@@ -308,96 +309,93 @@ def tile_hopfieldmodel_pa_s_kernel(tc, q_state, keys, W_lin, b_lin, out):
         regroup_keys(0, 0, "vector")
         transpose_keys(0, 0)
         warm_plain()
-        regroup_keys(0, 1, "vector")
         store_keys_t(0, 0, "scalar")
-        transpose_keys(0, 1)
-        warm_plain()
-        quantise_keys(0)
-        store_keys_t(0, 1, "scalar")
         transpose_q()
         warm_plain()
+        regroup_keys(0, 1, "vector")
         store_q_t("scalar")
-        regroup_keys(1, 0, "vector")
-        transpose_keys(1, 0)
+        transpose_keys(0, 1)
         warm_plain()
+        regroup_keys(1, 0, "vector")
+        store_keys_t(0, 1, "scalar")
+        transpose_keys(1, 0)
+        score(0, 0)
         regroup_keys(1, 1, "vector")
         store_keys_t(1, 0, "scalar")
+        warm_plain()
+        quantise_keys(0)
         transpose_keys(1, 1)
-        score(0, 0)
+        score(0, 1)
         quantise_keys(1)
         store_keys_t(1, 1, "scalar")
         transpose_keys(2, 0)
-        regroup_keys(2, 0, "vector")
-        score(0, 1)
-        store_keys_t(2, 0, "scalar")
-        transpose_keys(2, 1)
         bank_maximum(0, 0)
         regroup_keys(3, 0, "gpsimd")
-        transpose_keys(3, 0)
-        store_keys_t(2, 1, "scalar")
-        bank_maximum(0, 1)
+        transpose_keys(2, 1)
+        store_keys_t(2, 0, "scalar")
         score(1, 0)
-        transpose_keys(3, 1)
-        regroup_keys(3, 1, "gpsimd")
-        store_keys_t(3, 0, "vector")
-        exponentiate(0, 0)
+        bank_maximum(0, 1)
+        store_keys_t(2, 1, "scalar")
+        transpose_keys(3, 0)
         score(1, 1)
         bank_maximum(1, 0)
+        regroup_keys(3, 1, "gpsimd")
+        exponentiate(0, 0)
+        transpose_keys(3, 1)
+        bank_maximum(1, 1)
         exponentiate(0, 1)
         score(2, 0)
-        bank_maximum(1, 1)
-        regroup_keys(2, 1, "gpsimd")
+        regroup_keys(2, 0, "gpsimd")
+        store_keys_t(3, 0, "vector")
         store_keys_t(3, 1, "scalar")
         score(2, 1)
         bank_maximum(2, 0)
-        transpose_e(0)
         exponentiate(1, 0)
-        bank_maximum(2, 1)
+        transpose_e(0)
         exponentiate(1, 1)
+        bank_maximum(2, 1)
+        regroup_keys(2, 1, "gpsimd")
         score(3, 0)
-        quantise_keys(2)
         store_e_t(0, "scalar")
         score(3, 1)
+        invert_sums(0)
+        bank_maximum(3, 0)
         exponentiate(2, 0)
         transpose_e(1)
-        quantise_e(0)
-        invert_sums(0)
-        exponentiate(2, 1)
-        bank_maximum(3, 0)
-        spread_inverses(0)
-        retrieve(0)
-        store_e_t(1, "scalar")
-        bank_maximum(3, 1)
+        regroup_w("gpsimd")
         warm_mx()
-        transpose_e(2)
-        store_spread(0, "scalar")
-        regroup_w("vector")
+        bank_maximum(3, 1)
+        exponentiate(2, 1)
         warm_mx()
         exponentiate(3, 0)
-        quantise_e(1)
+        transpose_e(2)
+        quantise_e(0)
+        spread_inverses(0)
         exponentiate(3, 1)
+        quantise_keys(2)
+        retrieve(0)
+        warm_mx()
+        store_e_t(1, "scalar")
         quantise_keys(3)
-        retrieve(1)
-        store_e_t(2, "scalar")
-        warm_mx()
-        invert_sums(2)
-        hidden_pair(0)
-        warm_mx()
         transpose_e(3)
-        quantise_e(2)
-        warm_mx()
-        quantise_hidden(0)
-        store_e_t(3, "scalar")
+        store_e_t(2, "scalar")
+        invert_sums(2)
+        quantise_e(1)
         spread_inverses(2)
-        warm_mx()
+        store_spread(0, "scalar")
+        quantise_e(2)
+        retrieve(1)
+        store_e_t(3, "scalar")
+        quantise_w()
         retrieve(2)
         store_spread(2, "scalar")
         quantise_e(3)
-        quantise_w()
+        hidden_pair(0)
         retrieve(3)
         warm_mx()
-        hidden_pair(2)
+        quantise_hidden(0)
         warm_mx()
+        hidden_pair(2)
         quantise_hidden(1)
 
         y_ps = ps_s.tile([P, C], F32, tag="s")

@@ -315,80 +315,79 @@ def tile_hopfieldmodel_pa_s_kernel(tc, q_state, keys, W_lin, b_lin, out):
         regroup_keys(0, 1, "vector")
         store_q_t("scalar")
         transpose_keys(0, 1)
-        warm_plain()
         regroup_keys(1, 0, "vector")
-        store_keys_t(0, 1, "scalar")
         transpose_keys(1, 0)
-        score(0, 0)
-        regroup_keys(1, 1, "vector")
-        store_keys_t(1, 0, "scalar")
+        store_keys_t(0, 1, "scalar")
         warm_plain()
-        quantise_keys(0)
+        regroup_keys(1, 1, "vector")
         transpose_keys(1, 1)
-        score(0, 1)
-        quantise_keys(1)
+        store_keys_t(1, 0, "scalar")
+        score(0, 0)
+        quantise_keys(0)
         store_keys_t(1, 1, "scalar")
         transpose_keys(2, 0)
         bank_maximum(0, 0)
-        regroup_keys(3, 0, "gpsimd")
-        transpose_keys(2, 1)
+        regroup_keys(2, 1, "gpsimd")
+        score(0, 1)
         store_keys_t(2, 0, "scalar")
-        score(1, 0)
+        transpose_keys(2, 1)
         bank_maximum(0, 1)
+        score(1, 0)
         store_keys_t(2, 1, "scalar")
-        transpose_keys(3, 0)
+        regroup_keys(2, 0, "gpsimd")
         score(1, 1)
         bank_maximum(1, 0)
-        regroup_keys(3, 1, "gpsimd")
         exponentiate(0, 0)
+        transpose_keys(3, 0)
+        exponentiate(0, 1)
         transpose_keys(3, 1)
         bank_maximum(1, 1)
-        exponentiate(0, 1)
+        regroup_keys(3, 0, "gpsimd")
         score(2, 0)
-        regroup_keys(2, 0, "gpsimd")
-        store_keys_t(3, 0, "vector")
         store_keys_t(3, 1, "scalar")
+        store_keys_t(3, 0, "vector")
         score(2, 1)
-        bank_maximum(2, 0)
         exponentiate(1, 0)
+        bank_maximum(2, 0)
         transpose_e(0)
+        regroup_keys(3, 1, "gpsimd")
         exponentiate(1, 1)
-        bank_maximum(2, 1)
-        regroup_keys(2, 1, "gpsimd")
         score(3, 0)
+        bank_maximum(2, 1)
         store_e_t(0, "scalar")
         score(3, 1)
         invert_sums(0)
         bank_maximum(3, 0)
+        regroup_w("gpsimd")
         exponentiate(2, 0)
         transpose_e(1)
-        regroup_w("gpsimd")
         warm_mx()
         bank_maximum(3, 1)
         exponentiate(2, 1)
         warm_mx()
+        quantise_e(0)
         exponentiate(3, 0)
         transpose_e(2)
-        quantise_e(0)
-        spread_inverses(0)
+        quantise_keys(1)
         exponentiate(3, 1)
-        quantise_keys(2)
+        spread_inverses(0)
         retrieve(0)
+        quantise_keys(2)
         warm_mx()
         store_e_t(1, "scalar")
-        quantise_keys(3)
         transpose_e(3)
+        quantise_keys(3)
         store_e_t(2, "scalar")
         invert_sums(2)
+        store_spread(0, "scalar")
         quantise_e(1)
         spread_inverses(2)
-        store_spread(0, "scalar")
+        store_e_t(3, "scalar")
         quantise_e(2)
         retrieve(1)
-        store_e_t(3, "scalar")
         quantise_w()
-        retrieve(2)
         store_spread(2, "scalar")
+        retrieve(2)
         quantise_e(3)
         hidden_pair(0)
         retrieve(3)

@@ -21,7 +21,10 @@ PACK = 4
 K_PASS = P * PACK
 PASSES = K // K_PASS
 E_HALVES = E // P
-PAIR = 2
+PAIR = NETS // PASSES
+PAIR_STARTS = range(0, NETS, PAIR)
+RUN = 4
+HEAD_WARM_UPS = 4
 
 LN_TERMS = 26
 EXPONENT_BITS = 0x7F800000
@@ -45,16 +48,14 @@ def tile_hopfieldmodel_pa_s_kernel(tc, q_state, keys, W_lin, b_lin, out):
         q_sb = const.tile([P, NETS, E], BF16)
         w_sb = const.tile([P, PASSES, PACK, C], BF16)
         bias_sb = const.tile([P, C], BF16)
-
-        def keys_view(n):
-            return keys[n].rearrange("(g p j) e -> p g j e", g=PASSES, j=PACK)
-
-        nc.sync.dma_start(out=keys_sb[0][:, 0], in_=keys_view(0)[:, 0])
-        nc.sync.dma_start(out=q_sb[:], in_=q_state.rearrange("n b e -> b n e"))
-        nc.sync.dma_start(out=keys_sb[0][:, 1], in_=keys_view(0)[:, 1])
-        for n in range(1, NETS):
+        for n in range(NETS):
             for g in range(PASSES):
-                nc.sync.dma_start(out=keys_sb[n][:, g], in_=keys_view(n)[:, g])
+                nc.sync.dma_start(
+                    out=keys_sb[n][:, g],
+                    in_=keys[n].rearrange("(g p j) e -> p g j e", g=PASSES, j=PACK)[:, g],
+                )
+                if n == 0 and g == 0:
+                    nc.sync.dma_start(out=q_sb[:], in_=q_state.rearrange("n b e -> b n e"))
         nc.sync.dma_start(
             out=w_sb[:], in_=W_lin.rearrange("(g t p) c -> p g t c", g=PASSES, t=PACK)
         )
@@ -64,33 +65,10 @@ def tile_hopfieldmodel_pa_s_kernel(tc, q_state, keys, W_lin, b_lin, out):
         nc.vector.memset(zeros[:], 0.0)
         ident = const.tile([P, P], F32)
         make_identity(nc, ident[:])
-
         ln_terms = const.tile([P, LN_TERMS + 1], F32)
         for i in range(1, LN_TERMS + 1):
             c = LN_TERMS - i
             nc.vector.memset(ln_terms[:, c : c + 1], 0.25**i / i)
-
-        warm_ps = {}
-
-        def warm_plain():
-            if "plain" not in warm_ps:
-                warm_ps["plain"] = ps_s.tile([P, P], F32, tag="s", name="warm_plain_ps")
-            nc.tensor.matmul(
-                out=warm_ps["plain"][:], lhsT=zeros[:], rhs=zeros[:], start=True, stop=True
-            )
-
-        def warm_mx():
-            if "mx" not in warm_ps:
-                warm_ps["mx"] = ps_s.tile([P, PASSES * E], F32, tag="s", name="warm_mx_ps")
-            nc.tensor.matmul_mx(
-                out=warm_ps["mx"][:],
-                lhsT=k_codes[0][:, 0, :P].bitcast(FP8X4),
-                lhsT_scale=k_scales[0][:, 0, :P],
-                rhs=k_codes[0][:].rearrange("p g e -> p (g e)").bitcast(FP8X4),
-                rhs_scale=k_scales[0][:].rearrange("p g e -> p (g e)"),
-                start=True,
-                stop=True,
-            )
 
         q_t = const.tile([P, NETS, B], F32)
         keys_t = [const.tile([P, PASSES, K_PASS], F32, name="keys_t%d" % n) for n in range(NETS)]
@@ -104,57 +82,69 @@ def tile_hopfieldmodel_pa_s_kernel(tc, q_state, keys, W_lin, b_lin, out):
         e_sb = [const.tile([P, PASSES, K_PASS], BF16, name="e_sb%d" % n) for n in range(NETS)]
         row_sum = const.tile([P, NETS], F32)
         inv_sum = const.tile([P, NETS], F32)
-        inv_spread = {n: const.tile([P, B, PAIR], F32, name="inv_spread%d" % n) for n in range(0, NETS, PAIR)}
+        inv_spread = {
+            first: const.tile([P, B, PAIR], F32, name="inv_spread%d" % first)
+            for first in PAIR_STARTS
+        }
         w_grouped = const.tile([P, PASSES, C, PACK], BF16, align_bytes=64)
         w_codes = const.tile([P, PASSES, C], U32, align_bytes=64)
         w_scales = const.tile([P, PASSES, C], U8, align_bytes=64)
         h_grouped = const.tile([P, PASSES, B, PACK], BF16, align_bytes=64)
         h_codes = const.tile([P, PASSES, B], U32, align_bytes=64)
         h_scales = const.tile([P, PASSES, B], U8, align_bytes=64)
-        kt_ps, scores, e_t, e_grouped, spread_ps = {}, {}, {}, {}, {}
+        keys_t_ps, scores, e_t_ps, e_grouped, spread_ps = {}, {}, {}, {}, {}
         k_codes, k_scales, e_codes, e_scales, retrieved = {}, {}, {}, {}, {}
 
-        def copy_on(engine, out, in_):
-            if engine == "scalar":
-                nc.scalar.copy(out=out, in_=in_)
-            elif engine == "vector":
-                nc.vector.tensor_copy(out=out, in_=in_)
-            else:
-                nc.gpsimd.tensor_scalar(
-                    out=out, in0=in_, scalar1=1.0, scalar2=0.0, op0=ALU.mult, op1=ALU.add
-                )
+        plain_warm_ps = ps_s.tile([P, P], F32, tag="s")
+
+        def warm_plain():
+            nc.tensor.matmul(
+                out=plain_warm_ps[:], lhsT=zeros[:], rhs=zeros[:], start=True, stop=True
+            )
+
+        def warm_mx(mx_warm_ps):
+            nc.tensor.matmul_mx(
+                out=mx_warm_ps[:],
+                lhsT=k_codes[0][:, 0, :P].bitcast(FP8X4),
+                lhsT_scale=k_scales[0][:, 0, :P],
+                rhs=k_codes[0][:].rearrange("p g e -> p (g e)").bitcast(FP8X4),
+                rhs_scale=k_scales[0][:].rearrange("p g e -> p (g e)"),
+                start=True,
+                stop=True,
+            )
 
         def transpose_q():
-            qt_ps = ps_t.tile([P, NETS, B], F32, tag="t")
+            q_t_ps = ps_t.tile([P, NETS, B], F32, tag="t")
             for n in range(NETS):
                 nc.tensor.transpose(
-                    out=qt_ps[:, n, :], in_=q_sb[:, n, :].bitcast(F32), identity=ident[:]
+                    out=q_t_ps[:, n, :], in_=q_sb[:, n, :].bitcast(F32), identity=ident[:]
                 )
-            kt_ps["q"] = qt_ps
+            return q_t_ps
 
-        def store_q_t(engine):
-            copy_on(engine, q_t[:], kt_ps["q"][:])
+        def store_q_t(q_t_ps, first):
+            nets = slice(first, first + PAIR)
+            nc.scalar.copy(out=q_t[:, nets, :], in_=q_t_ps[:, nets, :])
 
         def transpose_keys(n, g):
-            ps = ps_t.tile([P, PACK, P], F32, tag="t")
+            keys_t_ps[(n, g)] = ps_t.tile([P, PACK, P], F32, tag="t", name="keys_t_ps")
             for j in range(PACK):
                 nc.tensor.transpose(
-                    out=ps[:, j, :], in_=keys_sb[n][:, g, j, :].bitcast(F32), identity=ident[:]
+                    out=keys_t_ps[(n, g)][:, j, :],
+                    in_=keys_sb[n][:, g, j, :].bitcast(F32),
+                    identity=ident[:],
                 )
-            kt_ps[(n, g)] = ps
 
-        def store_keys_t(n, g, engine):
-            copy_on(
-                engine,
-                keys_t[n][:, g, :].rearrange("w (u p i) -> w u p i", u=2, i=2),
-                kt_ps[(n, g)][:].rearrange("w (u i) p -> w u p i", i=2),
+        def store_keys_t(copy, n, g):
+            copy(
+                out=keys_t[n][:, g, :].rearrange("w (u p i) -> w u p i", u=2, i=2),
+                in_=keys_t_ps[(n, g)][:].rearrange("w (u i) p -> w u p i", i=2),
             )
 
         def score(n, g):
-            s_ps = ps_s.tile([P, K_PASS], F32, tag="s")
+            scores[(n, g)] = ps_s.tile([P, K_PASS], F32, tag="s", name="scores_ps")
             for parity in range(2):
                 nc.tensor.matmul(
-                    out=s_ps[:],
+                    out=scores[(n, g)][:],
                     lhsT=q_t[:, n, :].bitcast(BF16).rearrange("w (b i) -> w b i", i=2)[
                         :, :, parity
                     ],
@@ -164,17 +154,12 @@ def tile_hopfieldmodel_pa_s_kernel(tc, q_state, keys, W_lin, b_lin, out):
                     start=(parity == 0),
                     stop=(parity == 1),
                 )
-            scores[(n, g)] = s_ps
 
-        def regroup_keys(n, g, engine):
-            if engine == "vector":
-                copy_on(
-                    engine,
-                    k_grouped[n][:, g].rearrange("p (c i) j -> p c j i", i=4),
-                    keys_sb[n][:, g].rearrange("p j (c i) -> p c j i", i=4),
-                )
-            else:
-                copy_on(engine, k_grouped[n][:, g], keys_sb[n][:, g].rearrange("p j e -> p e j"))
+        def regroup_keys_on_vector(n, g):
+            nc.vector.tensor_copy(
+                out=k_grouped[n][:, g].rearrange("p (c i) j -> p c j i", i=RUN),
+                in_=keys_sb[n][:, g].rearrange("p j (c i) -> p c j i", i=RUN),
+            )
 
         def quantise_keys(n):
             k_codes[n] = per_net.tile([P, PASSES, E], U32, align_bytes=64, tag="k_codes", name="kc")
@@ -185,7 +170,7 @@ def tile_hopfieldmodel_pa_s_kernel(tc, q_state, keys, W_lin, b_lin, out):
                 in_=k_grouped[n][:].rearrange("p g e j -> p (g e j)"),
             )
 
-        def bank_maximum(n, g):
+        def take_maximum(n, g):
             nc.vector.tensor_scalar(
                 out=scaled_scores[:],
                 in0=scores[(n, g)][:],
@@ -207,25 +192,24 @@ def tile_hopfieldmodel_pa_s_kernel(tc, q_state, keys, W_lin, b_lin, out):
             )
 
         def transpose_e(n):
-            e_t[n] = ps_t.tile([P, PASSES, 2, B], F32, tag="t", name="et_ps")
+            e_t_ps[n] = ps_t.tile([P, PASSES, 2, B], F32, tag="t", name="e_t_ps")
             for g in range(PASSES):
                 for u in range(2):
                     nc.tensor.transpose(
-                        out=e_t[n][:, g, u, :],
+                        out=e_t_ps[n][:, g, u, :],
                         in_=e_sb[n][:, g, :].bitcast(F32)[:, u * P : (u + 1) * P],
                         identity=ident[:],
                     )
 
-        def store_e_t(n, engine):
+        def store_e_t(n):
             e_grouped[n] = per_net.tile(
                 [P, PASSES, B, PACK], BF16, align_bytes=64, tag="e_grouped", name="e_grouped"
             )
-            copy_on(
-                engine,
-                e_grouped[n][:].rearrange("p g b j -> p g (b j)").bitcast(F32).rearrange(
+            nc.scalar.copy(
+                out=e_grouped[n][:].rearrange("p g b j -> p g (b j)").bitcast(F32).rearrange(
                     "p g (b u) -> p g b u", u=2
                 ),
-                e_t[n][:].rearrange("p g u b -> p g b u"),
+                in_=e_t_ps[n][:].rearrange("p g u b -> p g b u"),
             )
 
         def quantise_e(n):
@@ -238,14 +222,16 @@ def tile_hopfieldmodel_pa_s_kernel(tc, q_state, keys, W_lin, b_lin, out):
             )
 
         def retrieve(n):
-            if n % PAIR == 0:
-                retrieved[n] = ps_s.tile([P, PAIR, E_HALVES, B], F32, tag="s", name="rt_ps")
-            rt_ps = retrieved[n - n % PAIR]
+            first, i = n - n % PAIR, n % PAIR
+            if i == 0:
+                retrieved[first] = ps_s.tile(
+                    [P, PAIR, E_HALVES, B], F32, tag="s", name="retrieved_ps"
+                )
             for half in range(E_HALVES):
                 cols = slice(half * P, (half + 1) * P)
                 for g in range(PASSES):
                     nc.tensor.matmul_mx(
-                        out=rt_ps[:, n % PAIR, half, :],
+                        out=retrieved[first][:, i, half, :],
                         lhsT=k_codes[n][:, g, cols].bitcast(FP8X4),
                         lhsT_scale=k_scales[n][:, g, cols],
                         rhs=e_codes[n][:, g, :].bitcast(FP8X4),
@@ -254,12 +240,18 @@ def tile_hopfieldmodel_pa_s_kernel(tc, q_state, keys, W_lin, b_lin, out):
                         stop=(g == PASSES - 1),
                     )
 
-        def invert_sums(first):
-            pair = slice(first, first + PAIR)
+        def sum_rows(first):
             nc.vector.tensor_reduce(
-                out=row_sum[:, pair], in_=bank_sum[:, pair, :], axis=AX.X, op=ALU.add
+                out=row_sum[:, first : first + PAIR],
+                in_=bank_sum[:, first : first + PAIR, :],
+                axis=AX.X,
+                op=ALU.add,
             )
-            nc.vector.reciprocal(out=inv_sum[:, pair], in_=row_sum[:, pair])
+
+        def invert_sums(first):
+            nc.vector.reciprocal(
+                out=inv_sum[:, first : first + PAIR], in_=row_sum[:, first : first + PAIR]
+            )
 
         def spread_inverses(first):
             spread_ps[first] = ps_t.tile([P, PAIR, B], F32, tag="t", name="spread_ps")
@@ -270,13 +262,10 @@ def tile_hopfieldmodel_pa_s_kernel(tc, q_state, keys, W_lin, b_lin, out):
                     identity=ident[:],
                 )
 
-        def store_spread(first, engine):
-            copy_on(
-                engine, inv_spread[first][:], spread_ps[first][:].rearrange("p n b -> p b n")
+        def store_spread(first):
+            nc.scalar.copy(
+                out=inv_spread[first][:], in_=spread_ps[first][:].rearrange("p i b -> p b i")
             )
-
-        def regroup_w(engine):
-            copy_on(engine, w_grouped[:], w_sb[:].rearrange("p g t c -> p g c t"))
 
         def quantise_w():
             nc.vector.quantize_mx(
@@ -285,7 +274,7 @@ def tile_hopfieldmodel_pa_s_kernel(tc, q_state, keys, W_lin, b_lin, out):
                 in_=w_grouped[:].rearrange("p g c t -> p (g c t)"),
             )
 
-        def hidden_pair(first):
+        def relu_and_divide(first):
             nc.vector.scalar_tensor_tensor(
                 out=h_grouped[:, first // PAIR].rearrange("p b (i t) -> p b i t", i=PAIR),
                 in0=retrieved[first][:].rearrange("p i t b -> p b i t"),
@@ -295,107 +284,107 @@ def tile_hopfieldmodel_pa_s_kernel(tc, q_state, keys, W_lin, b_lin, out):
                 op1=ALU.mult,
             )
 
-        def quantise_hidden(g):
+        def quantise_h(g):
             nc.vector.quantize_mx(
                 out=h_codes[:, g, :].bitcast(FP8X4),
                 scales=h_scales[:, g, :],
                 in_=h_grouped[:, g].rearrange("p b t -> p (b t)"),
             )
 
-        warm_plain()
-        warm_plain()
-        warm_plain()
-        warm_plain()
-        regroup_keys(0, 0, "vector")
+        for i in range(HEAD_WARM_UPS):
+            warm_plain()
         transpose_keys(0, 0)
+        store_keys_t(nc.scalar.copy, 0, 0)
+        regroup_keys_on_vector(0, 0)
         warm_plain()
-        store_keys_t(0, 0, "scalar")
-        transpose_q()
+        q_t_ps = transpose_q()
+        store_q_t(q_t_ps, 0)
         warm_plain()
-        regroup_keys(0, 1, "vector")
-        store_q_t("scalar")
         transpose_keys(0, 1)
-        regroup_keys(1, 0, "vector")
-        transpose_keys(1, 0)
-        store_keys_t(0, 1, "scalar")
-        warm_plain()
-        regroup_keys(1, 1, "vector")
-        transpose_keys(1, 1)
-        store_keys_t(1, 0, "scalar")
-        score(0, 0)
+        store_keys_t(nc.scalar.copy, 0, 1)
+        store_q_t(q_t_ps, PAIR)
+        regroup_keys_on_vector(0, 1)
+        for g in range(PASSES):
+            transpose_keys(1, g)
+            store_keys_t(nc.scalar.copy, 1, g)
+            score(0, g)
+        regroup_keys_on_vector(1, 0)
         quantise_keys(0)
-        store_keys_t(1, 1, "scalar")
+
+        for n, g in ((2, 0), (2, 1), (3, 0), (3, 1), (1, 1)):
+            nc.gpsimd.tensor_scalar(
+                out=k_grouped[n][:, g],
+                in0=keys_sb[n][:, g].rearrange("p j e -> p e j"),
+                scalar1=1.0,
+                scalar2=0.0,
+                op0=ALU.mult,
+                op1=ALU.add,
+            )
+
         transpose_keys(2, 0)
-        bank_maximum(0, 0)
-        regroup_keys(2, 1, "gpsimd")
-        score(0, 1)
-        store_keys_t(2, 0, "scalar")
+        store_keys_t(nc.scalar.copy, 2, 0)
+        for g in range(PASSES):
+            score(1, g)
+            take_maximum(0, g)
+        for g in range(PASSES):
+            exponentiate(0, g)
+        take_maximum(1, 0)
         transpose_keys(2, 1)
-        bank_maximum(0, 1)
-        score(1, 0)
-        store_keys_t(2, 1, "scalar")
-        regroup_keys(2, 0, "gpsimd")
-        score(1, 1)
-        bank_maximum(1, 0)
-        exponentiate(0, 0)
+        store_keys_t(nc.vector.tensor_copy, 2, 1)
+        take_maximum(1, 1)
         transpose_keys(3, 0)
-        exponentiate(0, 1)
-        transpose_keys(3, 1)
-        bank_maximum(1, 1)
-        regroup_keys(3, 0, "gpsimd")
+        store_keys_t(nc.scalar.copy, 3, 0)
         score(2, 0)
-        store_keys_t(3, 1, "scalar")
-        store_keys_t(3, 0, "vector")
-        score(2, 1)
-        exponentiate(1, 0)
-        bank_maximum(2, 0)
+        take_maximum(2, 0)
+        transpose_keys(3, 1)
+        store_keys_t(nc.vector.tensor_copy, 3, 1)
         transpose_e(0)
-        regroup_keys(3, 1, "gpsimd")
-        exponentiate(1, 1)
-        score(3, 0)
-        bank_maximum(2, 1)
-        store_e_t(0, "scalar")
-        score(3, 1)
-        invert_sums(0)
-        bank_maximum(3, 0)
-        regroup_w("gpsimd")
-        exponentiate(2, 0)
+        score(2, 1)
+        take_maximum(2, 1)
+        for g in range(PASSES):
+            exponentiate(1, g)
+        store_e_t(0)
+        for g in range(PASSES):
+            score(3, g)
+            exponentiate(2, g)
         transpose_e(1)
-        warm_mx()
-        bank_maximum(3, 1)
-        exponentiate(2, 1)
-        warm_mx()
-        quantise_e(0)
-        exponentiate(3, 0)
+        take_maximum(3, 0)
+        sum_rows(0)
+        take_maximum(3, 1)
+        invert_sums(0)
+        for g in range(PASSES):
+            exponentiate(3, g)
+
+        mx_warm_ps = ps_s.tile([P, PASSES * E], F32, tag="s")
+        for i in range(2):
+            warm_mx(mx_warm_ps)
         transpose_e(2)
-        quantise_keys(1)
-        exponentiate(3, 1)
         spread_inverses(0)
+        quantise_e(0)
         retrieve(0)
-        quantise_keys(2)
-        warm_mx()
-        store_e_t(1, "scalar")
+        warm_mx(mx_warm_ps)
         transpose_e(3)
+        quantise_keys(1)
+        quantise_keys(2)
+        sum_rows(2)
         quantise_keys(3)
-        store_e_t(2, "scalar")
         invert_sums(2)
-        store_spread(0, "scalar")
-        quantise_e(1)
         spread_inverses(2)
-        store_e_t(3, "scalar")
-        quantise_e(2)
-        retrieve(1)
+        for n in range(1, NETS):
+            store_e_t(n)
+            quantise_e(n)
+            retrieve(n)
+        for i in range(2):
+            warm_mx(mx_warm_ps)
+        for first in PAIR_STARTS:
+            store_spread(first)
+        nc.scalar.copy(out=w_grouped[:], in_=w_sb[:].rearrange("p g t c -> p g c t"))
+
+        for first in PAIR_STARTS:
+            relu_and_divide(first)
         quantise_w()
-        store_spread(2, "scalar")
-        retrieve(2)
-        quantise_e(3)
-        hidden_pair(0)
-        retrieve(3)
-        warm_mx()
-        quantise_hidden(0)
-        warm_mx()
-        hidden_pair(2)
-        quantise_hidden(1)
+        for g in range(PASSES):
+            quantise_h(g)
 
         y_ps = ps_s.tile([P, C], F32, tag="s")
         for g in range(PASSES):

import math
from contextlib import ExitStack

import concourse.mybir as mybir
from concourse.masks import make_identity

F32 = mybir.dt.float32
BF16 = mybir.dt.bfloat16
I32 = mybir.dt.int32
U32 = mybir.dt.uint32
U8 = mybir.dt.uint8
FP8X4 = mybir.dt.float8_e4m3fn_x4
ACT = mybir.ActivationFunctionType
ALU = mybir.AluOpType
AX = mybir.AxisListType

NETS, B, K, E, C = 4, 128, 1024, 256, 128
BETA = 2.0
P = 128
PACK = 4
K_PASS = P * PACK
PASSES = K // K_PASS
E_HALVES = E // P
PAIR = NETS // PASSES
PAIR_STARTS = range(0, NETS, PAIR)
RUN = 4
HEAD_WARM_UPS = 4

LN_TERMS = 26
EXPONENT_BITS = 0x7F800000
SIGN_AND_EXPONENT = -(2**23)

FLOPS = 2 * NETS * B * K * E * 2 + 2 * B * NETS * E * C


def tile_hopfieldmodel_pa_s_kernel(tc, q_state, keys, W_lin, b_lin, out):
    nc = tc.nc
    with ExitStack() as ctx:
        const = ctx.enter_context(tc.tile_pool(name="const", bufs=1))
        per_net = ctx.enter_context(tc.tile_pool(name="per_net", bufs=NETS))
        ps_t = ctx.enter_context(tc.psum_pool(name="ps_t", bufs=4))
        ps_s = ctx.enter_context(tc.psum_pool(name="ps_s", bufs=4))
        ctx.enter_context(tc.manual_schedule())

        keys_sb = [
            const.tile([P, PASSES, PACK, E], BF16, name="keys_sb%d" % n) for n in range(NETS)
        ]
        q_sb = const.tile([P, NETS, E], BF16)
        w_sb = const.tile([P, PASSES, PACK, C], BF16)
        bias_sb = const.tile([P, C], BF16)
        for n in range(NETS):
            for g in range(PASSES):
                nc.sync.dma_start(
                    out=keys_sb[n][:, g],
                    in_=keys[n].rearrange("(g p j) e -> p g j e", g=PASSES, j=PACK)[:, g],
                )
                if n == 0 and g == 0:
                    nc.sync.dma_start(out=q_sb[:], in_=q_state.rearrange("n b e -> b n e"))
        nc.sync.dma_start(
            out=w_sb[:], in_=W_lin.rearrange("(g t p) c -> p g t c", g=PASSES, t=PACK)
        )
        nc.sync.dma_start(out=bias_sb[:], in_=b_lin.partition_broadcast(P))

        zeros = const.tile([P, P], F32)
        nc.vector.memset(zeros[:], 0.0)
        ident = const.tile([P, P], F32)
        make_identity(nc, ident[:])
        ln_terms = const.tile([P, LN_TERMS + 1], F32)
        for i in range(1, LN_TERMS + 1):
            c = LN_TERMS - i
            nc.vector.memset(ln_terms[:, c : c + 1], 0.25**i / i)

        q_t = const.tile([P, NETS, B], F32)
        keys_t = [const.tile([P, PASSES, K_PASS], F32, name="keys_t%d" % n) for n in range(NETS)]
        k_grouped = [
            const.tile([P, PASSES, E, PACK], BF16, align_bytes=64, name="k_grouped%d" % n)
            for n in range(NETS)
        ]
        bank_sum = const.tile([P, NETS, PASSES], F32)
        neg_max = const.tile([P, NETS, PASSES], F32)
        scaled_scores = const.tile([P, K_PASS], BF16)
        e_sb = [const.tile([P, PASSES, K_PASS], BF16, name="e_sb%d" % n) for n in range(NETS)]
        row_sum = const.tile([P, NETS], F32)
        inv_sum = const.tile([P, NETS], F32)
        inv_spread = {
            first: const.tile([P, B, PAIR], F32, name="inv_spread%d" % first)
            for first in PAIR_STARTS
        }
        w_grouped = const.tile([P, PASSES, C, PACK], BF16, align_bytes=64)
        w_codes = const.tile([P, PASSES, C], U32, align_bytes=64)
        w_scales = const.tile([P, PASSES, C], U8, align_bytes=64)
        h_grouped = const.tile([P, PASSES, B, PACK], BF16, align_bytes=64)
        h_codes = const.tile([P, PASSES, B], U32, align_bytes=64)
        h_scales = const.tile([P, PASSES, B], U8, align_bytes=64)
        keys_t_ps, scores, e_t_ps, e_grouped, spread_ps = {}, {}, {}, {}, {}
        k_codes, k_scales, e_codes, e_scales, retrieved = {}, {}, {}, {}, {}

        plain_warm_ps = ps_s.tile([P, P], F32, tag="s")

        def warm_plain():
            nc.tensor.matmul(
                out=plain_warm_ps[:], lhsT=zeros[:], rhs=zeros[:], start=True, stop=True
            )

        def warm_mx(mx_warm_ps):
            nc.tensor.matmul_mx(
                out=mx_warm_ps[:],
                lhsT=k_codes[0][:, 0, :P].bitcast(FP8X4),
                lhsT_scale=k_scales[0][:, 0, :P],
                rhs=k_codes[0][:].rearrange("p g e -> p (g e)").bitcast(FP8X4),
                rhs_scale=k_scales[0][:].rearrange("p g e -> p (g e)"),
                start=True,
                stop=True,
            )

        def transpose_q():
            q_t_ps = ps_t.tile([P, NETS, B], F32, tag="t")
            for n in range(NETS):
                nc.tensor.transpose(
                    out=q_t_ps[:, n, :], in_=q_sb[:, n, :].bitcast(F32), identity=ident[:]
                )
            return q_t_ps

        def store_q_t(q_t_ps, first):
            nets = slice(first, first + PAIR)
            nc.scalar.copy(out=q_t[:, nets, :], in_=q_t_ps[:, nets, :])

        def transpose_keys(n, g):
            keys_t_ps[(n, g)] = ps_t.tile([P, PACK, P], F32, tag="t", name="keys_t_ps")
            for j in range(PACK):
                nc.tensor.transpose(
                    out=keys_t_ps[(n, g)][:, j, :],
                    in_=keys_sb[n][:, g, j, :].bitcast(F32),
                    identity=ident[:],
                )

        def store_keys_t(copy, n, g):
            copy(
                out=keys_t[n][:, g, :].rearrange("w (u p i) -> w u p i", u=2, i=2),
                in_=keys_t_ps[(n, g)][:].rearrange("w (u i) p -> w u p i", i=2),
            )

        def score(n, g):
            scores[(n, g)] = ps_s.tile([P, K_PASS], F32, tag="s", name="scores_ps")
            for parity in range(2):
                nc.tensor.matmul(
                    out=scores[(n, g)][:],
                    lhsT=q_t[:, n, :].bitcast(BF16).rearrange("w (b i) -> w b i", i=2)[
                        :, :, parity
                    ],
                    rhs=keys_t[n][:, g, :].bitcast(BF16).rearrange("w (c i) -> w c i", i=2)[
                        :, :, parity
                    ],
                    start=(parity == 0),
                    stop=(parity == 1),
                )

        def regroup_keys_on_vector(n, g):
            nc.vector.tensor_copy(
                out=k_grouped[n][:, g].rearrange("p (c i) j -> p c j i", i=RUN),
                in_=keys_sb[n][:, g].rearrange("p j (c i) -> p c j i", i=RUN),
            )

        def quantise_keys(n):
            k_codes[n] = per_net.tile([P, PASSES, E], U32, align_bytes=64, tag="k_codes", name="kc")
            k_scales[n] = per_net.tile([P, PASSES, E], U8, align_bytes=64, tag="k_scales", name="ks")
            nc.vector.quantize_mx(
                out=k_codes[n][:].rearrange("p g e -> p (g e)").bitcast(FP8X4),
                scales=k_scales[n][:].rearrange("p g e -> p (g e)"),
                in_=k_grouped[n][:].rearrange("p g e j -> p (g e j)"),
            )

        def take_maximum(n, g):
            nc.vector.tensor_scalar(
                out=scaled_scores[:],
                in0=scores[(n, g)][:],
                scalar1=-BETA,
                scalar2=None if g == 0 else neg_max[:, n, g - 1 : g],
                op0=ALU.mult,
                op1=ALU.min,
                accum_out=neg_max[:, n, g : g + 1],
            )

        def exponentiate(n, g):
            nc.scalar.activation(
                out=e_sb[n][:, g, :],
                in_=scores[(n, g)][:],
                func=ACT.Exp,
                bias=neg_max[:, n, PASSES - 1 : PASSES],
                scale=BETA,
                accum_out=bank_sum[:, n, g : g + 1],
            )

        def transpose_e(n):
            e_t_ps[n] = ps_t.tile([P, PASSES, 2, B], F32, tag="t", name="e_t_ps")
            for g in range(PASSES):
                for u in range(2):
                    nc.tensor.transpose(
                        out=e_t_ps[n][:, g, u, :],
                        in_=e_sb[n][:, g, :].bitcast(F32)[:, u * P : (u + 1) * P],
                        identity=ident[:],
                    )

        def store_e_t(n):
            e_grouped[n] = per_net.tile(
                [P, PASSES, B, PACK], BF16, align_bytes=64, tag="e_grouped", name="e_grouped"
            )
            nc.scalar.copy(
                out=e_grouped[n][:].rearrange("p g b j -> p g (b j)").bitcast(F32).rearrange(
                    "p g (b u) -> p g b u", u=2
                ),
                in_=e_t_ps[n][:].rearrange("p g u b -> p g b u"),
            )

        def quantise_e(n):
            e_codes[n] = per_net.tile([P, PASSES, B], U32, align_bytes=64, tag="e_codes", name="ec")
            e_scales[n] = per_net.tile([P, PASSES, B], U8, align_bytes=64, tag="e_scales", name="es")
            nc.vector.quantize_mx(
                out=e_codes[n][:].rearrange("p g b -> p (g b)").bitcast(FP8X4),
                scales=e_scales[n][:].rearrange("p g b -> p (g b)"),
                in_=e_grouped[n][:].rearrange("p g b j -> p (g b j)"),
            )

        def retrieve(n):
            first, i = n - n % PAIR, n % PAIR
            if i == 0:
                retrieved[first] = ps_s.tile(
                    [P, PAIR, E_HALVES, B], F32, tag="s", name="retrieved_ps"
                )
            for half in range(E_HALVES):
                cols = slice(half * P, (half + 1) * P)
                for g in range(PASSES):
                    nc.tensor.matmul_mx(
                        out=retrieved[first][:, i, half, :],
                        lhsT=k_codes[n][:, g, cols].bitcast(FP8X4),
                        lhsT_scale=k_scales[n][:, g, cols],
                        rhs=e_codes[n][:, g, :].bitcast(FP8X4),
                        rhs_scale=e_scales[n][:, g, :],
                        start=(g == 0),
                        stop=(g == PASSES - 1),
                    )

        def sum_rows(first):
            nc.vector.tensor_reduce(
                out=row_sum[:, first : first + PAIR],
                in_=bank_sum[:, first : first + PAIR, :],
                axis=AX.X,
                op=ALU.add,
            )

        def invert_sums(first):
            nc.vector.reciprocal(
                out=inv_sum[:, first : first + PAIR], in_=row_sum[:, first : first + PAIR]
            )

        def spread_inverses(first):
            spread_ps[first] = ps_t.tile([P, PAIR, B], F32, tag="t", name="spread_ps")
            for i in range(PAIR):
                nc.tensor.transpose(
                    out=spread_ps[first][:, i, :],
                    in_=inv_sum[:, first + i : first + i + 1].to_broadcast([P, P]),
                    identity=ident[:],
                )

        def store_spread(first):
            nc.scalar.copy(
                out=inv_spread[first][:], in_=spread_ps[first][:].rearrange("p i b -> p b i")
            )

        def quantise_w():
            nc.vector.quantize_mx(
                out=w_codes[:].rearrange("p g c -> p (g c)").bitcast(FP8X4),
                scales=w_scales[:].rearrange("p g c -> p (g c)"),
                in_=w_grouped[:].rearrange("p g c t -> p (g c t)"),
            )

        def relu_and_divide(first):
            nc.vector.scalar_tensor_tensor(
                out=h_grouped[:, first // PAIR].rearrange("p b (i t) -> p b i t", i=PAIR),
                in0=retrieved[first][:].rearrange("p i t b -> p b i t"),
                scalar=0.0,
                in1=inv_spread[first][:].unsqueeze(3).to_broadcast([P, B, PAIR, E_HALVES]),
                op0=ALU.max,
                op1=ALU.mult,
            )

        def quantise_h(g):
            nc.vector.quantize_mx(
                out=h_codes[:, g, :].bitcast(FP8X4),
                scales=h_scales[:, g, :],
                in_=h_grouped[:, g].rearrange("p b t -> p (b t)"),
            )

        for i in range(HEAD_WARM_UPS):
            warm_plain()
        transpose_keys(0, 0)
        store_keys_t(nc.scalar.copy, 0, 0)
        regroup_keys_on_vector(0, 0)
        warm_plain()
        q_t_ps = transpose_q()
        store_q_t(q_t_ps, 0)
        warm_plain()
        transpose_keys(0, 1)
        store_keys_t(nc.scalar.copy, 0, 1)
        store_q_t(q_t_ps, PAIR)
        regroup_keys_on_vector(0, 1)
        for g in range(PASSES):
            transpose_keys(1, g)
            store_keys_t(nc.scalar.copy, 1, g)
            score(0, g)
        regroup_keys_on_vector(1, 0)
        quantise_keys(0)

        for n, g in ((2, 0), (2, 1), (3, 0), (3, 1), (1, 1)):
            nc.gpsimd.tensor_scalar(
                out=k_grouped[n][:, g],
                in0=keys_sb[n][:, g].rearrange("p j e -> p e j"),
                scalar1=1.0,
                scalar2=0.0,
                op0=ALU.mult,
                op1=ALU.add,
            )

        transpose_keys(2, 0)
        store_keys_t(nc.scalar.copy, 2, 0)
        for g in range(PASSES):
            score(1, g)
            take_maximum(0, g)
        for g in range(PASSES):
            exponentiate(0, g)
        take_maximum(1, 0)
        transpose_keys(2, 1)
        store_keys_t(nc.vector.tensor_copy, 2, 1)
        take_maximum(1, 1)
        transpose_keys(3, 0)
        store_keys_t(nc.scalar.copy, 3, 0)
        score(2, 0)
        take_maximum(2, 0)
        transpose_keys(3, 1)
        store_keys_t(nc.vector.tensor_copy, 3, 1)
        transpose_e(0)
        score(2, 1)
        take_maximum(2, 1)
        for g in range(PASSES):
            exponentiate(1, g)
        store_e_t(0)
        for g in range(PASSES):
            score(3, g)
            exponentiate(2, g)
        transpose_e(1)
        take_maximum(3, 0)
        sum_rows(0)
        take_maximum(3, 1)
        invert_sums(0)
        for g in range(PASSES):
            exponentiate(3, g)

        mx_warm_ps = ps_s.tile([P, PASSES * E], F32, tag="s")
        for i in range(2):
            warm_mx(mx_warm_ps)
        transpose_e(2)
        spread_inverses(0)
        quantise_e(0)
        retrieve(0)
        warm_mx(mx_warm_ps)
        transpose_e(3)
        quantise_keys(1)
        quantise_keys(2)
        sum_rows(2)
        quantise_keys(3)
        invert_sums(2)
        spread_inverses(2)
        for n in range(1, NETS):
            store_e_t(n)
            quantise_e(n)
            retrieve(n)
        for i in range(2):
            warm_mx(mx_warm_ps)
        for first in PAIR_STARTS:
            store_spread(first)
        nc.scalar.copy(out=w_grouped[:], in_=w_sb[:].rearrange("p g t c -> p g c t"))

        for first in PAIR_STARTS:
            relu_and_divide(first)
        quantise_w()
        for g in range(PASSES):
            quantise_h(g)

        y_ps = ps_s.tile([P, C], F32, tag="s")
        for g in range(PASSES):
            nc.tensor.matmul_mx(
                out=y_ps[:],
                lhsT=h_codes[:, g, :].bitcast(FP8X4),
                lhsT_scale=h_scales[:, g, :],
                rhs=w_codes[:, g, :].bitcast(FP8X4),
                rhs_scale=w_scales[:, g, :],
                start=(g == 0),
                stop=(g == PASSES - 1),
            )
        y = const.tile([P, C], F32)
        nc.vector.tensor_tensor(out=y[:], in0=y_ps[:], in1=bias_sb[:], op=ALU.add)
        neg_y_max = const.tile([P, 1], F32)
        nc.vector.tensor_reduce(out=neg_y_max[:], in_=y[:], axis=AX.X, op=ALU.max, negate=True)
        exp_shifted = const.tile([P, C], F32)
        exp_sum = const.tile([P, 1], F32)
        nc.scalar.activation(
            out=exp_shifted[:], in_=y[:], func=ACT.Exp, bias=neg_y_max[:], accum_out=exp_sum[:]
        )
        flipped = const.tile([P, 1], I32)
        nc.vector.tensor_scalar(
            out=flipped[:],
            in0=exp_sum[:].bitcast(I32),
            scalar1=EXPONENT_BITS,
            scalar2=SIGN_AND_EXPONENT,
            op0=ALU.bitwise_and,
            op1=ALU.bitwise_xor,
        )
        u4 = const.tile([P, 1], F32)
        nc.vector.tensor_scalar(
            out=u4[:],
            in0=exp_sum[:],
            scalar1=flipped[:].bitcast(F32),
            scalar2=4.0,
            op0=ALU.mult,
            op1=ALU.add,
        )
        nc.vector.tensor_scalar(
            out=ln_terms[:, LN_TERMS : LN_TERMS + 1],
            in0=flipped[:],
            scalar1=float(2**31 - 129 * 2**23),
            scalar2=math.log(2.0) / 2**23,
            op0=ALU.add,
            op1=ALU.mult,
        )
        neg_log = const.tile([P, LN_TERMS + 1], F32)
        nc.vector.tensor_tensor_scan(
            out=neg_log[:],
            data0=u4[:].to_broadcast([P, LN_TERMS + 1]),
            data1=ln_terms[:],
            initial=0.0,
            op0=ALU.mult,
            op1=ALU.add,
        )
        result = const.tile([P, C], F32)
        nc.vector.tensor_scalar(
            out=result[:],
            in0=y[:],
            scalar1=neg_y_max[:],
            scalar2=neg_log[:, LN_TERMS : LN_TERMS + 1],
            op0=ALU.add,
            op1=ALU.add,
        )
        nc.sync.dma_start(out=out, in_=result[:])
